import numpy as np
import ml_dtypes


def mxq(x, axis, fmt="e4m3"):
    dtype, down = {"e4m3": (ml_dtypes.float8_e4m3fn, 7), "e5m2": (ml_dtypes.float8_e5m2, 14)}[fmt]
    v = np.moveaxis(np.asarray(x, np.float32).astype(ml_dtypes.bfloat16).astype(np.float64), axis, -1)
    blocks = v.reshape(v.shape[:-1] + (-1, 32))
    amax = np.abs(blocks).max(-1, keepdims=True)
    byte = np.maximum(np.where(amax > 0, np.frexp(amax)[1] - 1 + 127, 0) - down, 1)
    scale = np.exp2(byte - 127.0)
    codes = (blocks / scale).astype(np.float32).astype(dtype).astype(np.float64)
    return np.moveaxis((codes * scale).reshape(v.shape), -1, axis)


WIDE = False


def mx_kscale(k):
    if not WIDE:
        return np.ones(k)
    levels = np.array([10, -10, 5, -5, 0])
    a = np.random.permutation(np.resize(levels, k // 512 * 4)).reshape(k // 512, 4)
    idx = np.arange(k)
    return np.exp2(a[idx // 512, idx % 128 // 32])


BF16 = ml_dtypes.bfloat16


def bf(x):
    return np.asarray(x, np.float32).astype(BF16)


def f64(x):
    return np.asarray(x).astype(np.float64)


BN, V, D, H, DEPTH, P = 256, 491, 16, 512, 4, 768
MD = V + D + 5
DH = D * H


def erf(v):
    a = np.clip(v, -6.0, 6.0)
    q = 2.0 * a * a
    term = a.copy()
    tot = a.copy()
    for n in range(1, 110):
        term = term * q / (2.0 * n + 1.0)
        tot = tot + term
    return 2.0 / np.sqrt(np.pi) * np.exp(-a * a) * tot


def gelu(v):
    return 0.5 * v * (1.0 + erf(v / np.sqrt(2.0)))


def ln(x, g, b):
    m = x.mean(-1, keepdims=True)
    v = ((x - m) ** 2).mean(-1, keepdims=True)
    return (x - m) / np.sqrt(v + 1e-5) * g + b


def setup_inputs():
    s = np.array(mx_kscale(MD), dtype=np.float64)
    s[V + 1 + D] = 1.0
    sU, sS, sV, sT = s[:V], s[V], s[V + 1:V + 1 + D], s[V + 1 + D:]
    t = mx_kscale(DH)[:H]
    c = np.concatenate([np.full(V, 0.8 / np.sqrt(V)), [0.3], np.full(D, 0.4 / np.sqrt(D)), [0.3, 0.3, 0.3, 0.3 / D]])
    cf = np.concatenate([np.tile(1.0 / (np.sqrt(DH) * t), D), [0.3, 0.3]])
    n = np.random.standard_normal
    u = np.random.random
    return {"U": bf(n((BN, V, D)) * sU[None, :, None]),
            "S": bf(u((BN, D)) * sS),
            "Vt": bf(n((BN, D, D)) * sV),
            "friction": bf(u((BN, D))),
            "settle": bf(u((BN, D)) * sT[1]),
            "char_coeffs": bf(n((BN, D)) * sT[2]),
            "ext_order": bf(u((BN, D)) * D * sT[3]),
            "refine_res": bf(n(BN)),
            "release_res": bf(n(BN)),
            "Wp": bf(n((H, MD)) * c / s),
            "bp": bf(n(H) * 0.2),
            "gp": bf((1.0 + 0.1 * n(H)) * t),
            "betap": bf(n(H) * 0.2 * t),
            "Wf": bf(n((H, DH + 2)) * cf),
            "bfuse": bf(n(H) * 0.2),
            "gf": bf(1.0 + 0.1 * n(H)),
            "betaf": bf(n(H) * 0.2)}


def reference(U, S, Vt, friction, settle, char_coeffs, ext_order, refine_res, release_res, Wp, bp, gp, betap, Wf, bfuse, gf, betaf):
    fr = np.log1p(f64(friction))
    bundle = np.concatenate([f64(U).transpose(0, 2, 1), f64(S)[..., None], f64(Vt), fr[..., None], f64(settle)[..., None],
                             f64(char_coeffs)[..., None], f64(ext_order)[..., None]], axis=-1)
    z1 = (mxq(bundle, 2, "e4m3") @ mxq(f64(Wp).T, 0, "e4m3")) + f64(bp)
    h_modes = ln(gelu(z1), f64(gp), f64(betap))
    wf = f64(Wf)
    z2 = mxq(h_modes.reshape(BN, DH), 1, "e4m3") @ mxq(wf[:, :DH].T, 0, "e4m3")
    z2 = z2 + f64(refine_res)[:, None] * wf[:, DH] + f64(release_res)[:, None] * wf[:, DH + 1] + f64(bfuse)
    return ln(gelu(z2), f64(gf), f64(betaf))

@@ -1,0 +1,456 @@
+from contextlib import ExitStack
+
+import concourse.mybir as mybir
+from concourse.masks import make_identity
+
+F32 = mybir.dt.float32
+BF16 = mybir.dt.bfloat16
+U32 = mybir.dt.uint32
+U8 = mybir.dt.uint8
+FP8X4 = mybir.dt.float8_e4m3fn_x4
+ACT = mybir.ActivationFunctionType
+ALU = mybir.AluOpType
+
+P = 128
+BN, V, D, H = 256, 491, 16, 512
+DH = D * H
+FLOPS = 2 * BN * D * H * H + 2 * BN * DH * H
+EPS = 1e-5
+NS = 8
+
+
+def tile_conduitdecoder_pa_kernel(
+    tc, U, S, Vt, friction, settle, char_coeffs, ext_order, refine_res, release_res,
+    Wp, bp, gp, betap, Wf, bfuse, gf, betaf, out,
+):
+    nc = tc.nc
+    with ExitStack() as ctx:
+        ctx.enter_context(tc.manual_schedule())
+        const = ctx.enter_context(tc.tile_pool(name="const", bufs=1))
+        keep = ctx.enter_context(tc.tile_pool(name="keep", bufs=1))
+        setup = ctx.enter_context(tc.tile_pool(name="setup", bufs=1))
+        wrp = ctx.enter_context(tc.tile_pool(name="wrp", bufs=4))
+        wgp = ctx.enter_context(tc.tile_pool(name="wgp", bufs=3))
+        xgp = ctx.enter_context(tc.tile_pool(name="xgp", bufs=2))
+        zbp = ctx.enter_context(tc.tile_pool(name="zbp", bufs=3))
+        gpl = ctx.enter_context(tc.tile_pool(name="gpl", bufs=8))
+        npl = ctx.enter_context(tc.tile_pool(name="npl", bufs=4))
+        mpp = ctx.enter_context(tc.tile_pool(name="mpp", bufs=2))
+        small = ctx.enter_context(tc.tile_pool(name="small", bufs=2))
+        psum = ctx.enter_context(tc.psum_pool(name="psum", bufs=1))
+
+        identF = const.tile([P, P], F32, name="identF")
+        make_identity(nc, identF[:])
+        XR = keep.tile([P, BN, 4, D], BF16, name="XR")
+        FR = setup.tile([P, BN * D], BF16, name="FR")
+        VtA = setup.tile([P, 2 * D * D], BF16, name="VtA")
+        VEC = setup.tile([P, 4, H], BF16, name="VEC")
+        GV = setup.tile([P, 256], BF16, name="GV")
+        RA = setup.tile([P, BN], BF16, name="RA")
+        WtIn = setup.tile([P, 4, P], BF16, name="WtIn")
+        ones = const.tile([P, P], BF16, name="ones")
+        neghalf = const.tile([P, 4], F32, name="neghalf")
+        nc.vector.memset(FR[96:127, :], 0.0)
+        nc.vector.memset(VEC[:], 0.0)
+        nc.vector.memset(GV[:], 0.0)
+        nc.vector.memset(ones[:], 1.0)
+        nc.vector.memset(RA[:], 0.0)
+        nc.vector.memset(WtIn[:], 0.0)
+        nc.vector.memset(neghalf[:], -0.5)
+
+        wf_rows = Wf.rearrange("(a p) c -> p a c", p=P)
+        out_flat = out.rearrange("a b -> (a b)")
+        WRt = []
+
+        def load_wf(c):
+            wr = wrp.tile([P, 4, 1024], BF16, name="wr")
+            nc.sync.dma_start(out=wr[:], in_=wf_rows[:, :, 1024 * c:1024 * c + 1024])
+            WRt.append(wr)
+
+        def load_u(s):
+            nc.sync.dma_start(
+                out=XR[0:96, 32 * s:32 * s + 32, :, :].rearrange("p b j k -> p b (j k)"),
+                in_=U[32 * s:32 * s + 32, 0:384, :].rearrange("b (p j) k -> p b (j k)", j=4),
+            )
+
+        def load_u_high(q):
+            b0, b1 = 64 * q, 64 * q + 64
+            for (p0, p1, v0, v1) in ((96, 120, 384, 480), (120, 122, 480, 488)):
+                nc.sync.dma_start(
+                    out=XR[p0:p1, b0:b1, :, :].rearrange("p b j k -> p b (j k)"),
+                    in_=U[b0:b1, v0:v1, :].rearrange("b (p j) k -> p b (j k)", j=4),
+                )
+            nc.sync.dma_start(
+                out=XR[122:123, b0:b1, 0:3, :].rearrange("p b j k -> p b (j k)"),
+                in_=U[b0:b1, 488:491, :].rearrange("b (p j) k -> p b (j k)", p=1),
+            )
+
+        def load_vt(b0, b1):
+            nc.sync.dma_start(
+                out=XR[123:127, b0:b1, :, :].rearrange("p b j k -> p (b j k)").bitcast(F32),
+                in_=out_flat[0:32768].rearrange("(q n) -> q n", q=4)[:, 32 * b0:32 * b1],
+            )
+
+        nc.sync.dma_start(out=FR[127:128, :], in_=friction.rearrange("(o b) k -> o (b k)", o=1))
+        nc.sync.dma_start(out=VtA[:], in_=Vt.rearrange("(p x) k d -> p (x k d)", x=2))
+        WpSb = wgp.tile([P, 4, H], BF16, name="WpSb", tag="wg", align_bytes=64)
+        for u in range(2):
+            nc.sync.dma_start(
+                out=WpSb[:, 2 * u:2 * u + 2, :],
+                in_=Wp[256 * u:256 * u + 256, :].rearrange("(p e) i -> p e i", e=2),
+            )
+        load_u(0)
+        load_wf(0)
+        for (pp, j, vec) in ((122, 3, S), (127, 1, settle), (127, 2, char_coeffs), (127, 3, ext_order)):
+            nc.gpsimd.dma_start(out=XR[pp:pp + 1, :, j, :], in_=vec.rearrange("(o b) k -> o b k", o=1))
+        nc.gpsimd.dma_start(out=VEC[0:1, 0, :], in_=bp.rearrange("(o n) -> o n", o=1))
+        nc.gpsimd.dma_start(out=GV[0:2, :], in_=gp.rearrange("(r c) -> r c", r=2))
+        nc.gpsimd.dma_start(out=GV[2:4, :], in_=betap.rearrange("(r c) -> r c", r=2))
+        identB = const.tile([P, P], BF16, name="identB")
+        make_identity(nc, identB[:])
+        for i, vec in ((1, gf), (2, betaf), (3, bfuse)):
+            nc.gpsimd.dma_start(out=VEC[0:1, i, :], in_=vec.rearrange("(o n) -> o n", o=1))
+        nc.gpsimd.dma_start(out=WtIn[:, :, 0:2], in_=wf_rows[:, :, DH:DH + 2])
+        nc.gpsimd.dma_start(out=RA[0:1, :], in_=refine_res.rearrange("(o n) -> o n", o=1))
+        nc.gpsimd.dma_start(out=RA[1:2, :], in_=release_res.rearrange("(o n) -> o n", o=1))
+
+        VtB = setup.tile([P, 4, 2, 4, D], BF16, name="VtB")
+        vta = VtA[:].rearrange("p (x k q j) -> p q x j k", x=2, k=D, q=4)
+        for q in range(4):
+            nc.vector.tensor_copy(out=VtB[:, q, :, :, :], in_=vta[:, q])
+        for q in range(4):
+            nc.scalar.activation(
+                out=XR[96:128, 64 * q:64 * q + 64, 0, :],
+                in_=FR[96:128, 1024 * q:1024 * q + 1024].rearrange("p (b k) -> p b k", k=D),
+                func=ACT.Ln, bias=1.0, scale=1.0,
+            )
+        nc.sync.dma_start(
+            out=out_flat[0:32768].rearrange("(q p w) -> p q w", q=4, p=P),
+            in_=VtB[:].rearrange("p q x j k -> p (q x j k)").bitcast(F32).rearrange("p (q w) -> p q w", q=4),
+        )
+        load_u_high(0)
+        load_vt(0, 64)
+        load_u(1)
+        load_wf(1)
+        load_vt(64, 256)
+        load_u(2)
+        load_u_high(1)
+        load_wf(2)
+        load_u(3)
+        load_wf(3)
+
+        def late_loads(i):
+            if i < 4:
+                load_u(4 + i)
+                if i % 2 == 0:
+                    load_u_high(2 + i // 2)
+                load_wf(4 + i)
+
+        WpC = const.tile([P, H], U32, name="WpC", align_bytes=64)
+        WpS = const.tile([P, H], U8, name="WpS", align_bytes=64)
+        WpG = wgp.tile([P, H, 4], BF16, name="WpG", tag="wg", align_bytes=64)
+        wp32 = WpSb[:].rearrange("p a i -> p (a i)").bitcast(F32).rearrange("p (a q w) -> p a q w", a=4, w=2)
+        wpg32 = WpG[:].rearrange("p n t -> p (n t)").bitcast(F32).rearrange("p (n w) -> p n w", w=2)
+        for hh in range(2):
+            pt = psum.tile([P, 2, 256], F32, name="pt", tag="wT", bufs=2)
+            for w in range(2):
+                for a in range(2):
+                    nc.tensor.transpose(out=pt[:, w, P * a:P * a + P], in_=wp32[:, 2 * hh + a, :, w], identity=identF[:])
+            nc.vector.tensor_copy(out=wpg32[:, 256 * hh:256 * hh + 256, :], in_=pt[:].rearrange("p w n -> p n w"))
+
+        nc.vector.quantize_mx(out=WpC[:].bitcast(FP8X4), scales=WpS[:], in_=WpG[:].rearrange("p n t -> p (n t)"))
+
+        bpB = const.tile([P, H], F32, name="bpB")
+        gfB = const.tile([P, H], F32, name="gfB")
+        betafB = const.tile([P, H], F32, name="betafB")
+        GB = const.tile([P, 8], F32, name="GB")
+        RB = setup.tile([P, H], BF16, name="RB")
+        Rsb = const.tile([P, 2, H], F32, name="Rsb")
+
+        def spread_bp():
+            pb = psum.tile([P, H], F32, name="pb", tag="nT0")
+            nc.tensor.matmul(out=pb[:], lhsT=ones[:], rhs=VEC[:, 0, :], start=True, stop=True)
+            nc.vector.tensor_copy(
+                out=bpB[:].rearrange("p (u e q) -> p u e q", u=2, e=2),
+                in_=pb[:].rearrange("p (u q e) -> p u e q", u=2, e=2),
+            )
+
+        def spread_rest():
+            pg = psum.tile([P, P], F32, name="pg", tag="nT1")
+            nc.tensor.transpose(out=pg[:], in_=GV[:].bitcast(F32), identity=identF[:])
+            nc.scalar.copy(out=GB[:], in_=pg[:, 0:4].bitcast(BF16))
+            pb2 = psum.tile([P, H], F32, name="pb2", tag="nT2")
+            nc.tensor.matmul(out=pb2[:], lhsT=ones[:], rhs=VEC[:, 1, :], start=True, stop=True)
+            nc.scalar.copy(out=gfB[:], in_=pb2[:])
+            pb3 = psum.tile([P, H], F32, name="pb3", tag="nT3")
+            nc.tensor.matmul(out=pb3[:], lhsT=ones[:], rhs=VEC[:, 2, :], start=True, stop=True)
+            nc.scalar.copy(out=betafB[:], in_=pb3[:])
+            pB = psum.tile([P, H], BF16, name="pB", tag="nT0")
+            for a in range(4):
+                nc.tensor.transpose(out=pB[:, P * a:P * a + P], in_=WtIn[:, a, :], identity=identB[:])
+            nc.scalar.copy(out=RB[:], in_=pB[:])
+            for bh in range(2):
+                pr = psum.tile([P, H], F32, name="pr", tag="nT%d" % (1 + bh))
+                nc.tensor.matmul(out=pr[:], lhsT=ones[:], rhs=VEC[:, 3, :], start=True, stop=False)
+                nc.tensor.matmul(out=pr[:], lhsT=RA[:, P * bh:P * bh + P], rhs=RB[:], start=False, stop=True)
+                nc.scalar.copy(out=Rsb[:, bh, :], in_=pr[:])
+
+        WC = keep.tile([P, D, H], U32, name="WC", align_bytes=64)
+        WS = keep.tile([P, D, H], U8, name="WS", align_bytes=64)
+        wps = {}
+        wgs = {}
+
+        def w_transposes(k):
+            c, half = divmod(k, 2)
+            wr32 = WRt[c][:].rearrange("p a c -> p (a c)").bitcast(F32).rearrange("p (a w) -> p a w", a=4)
+            tiles = []
+            for hh in range(2):
+                pt = psum.tile([P, 2, 256], F32, name="pt", tag="wT", bufs=2)
+                for u in range(2):
+                    for a in range(2):
+                        w0 = 256 * half + P * u
+                        nc.tensor.transpose(out=pt[:, u, P * a:P * a + P], in_=wr32[:, 2 * hh + a, w0:w0 + P], identity=identF[:])
+                tiles.append(pt)
+            wps[k] = tiles
+
+        def w_copies(k, second_on_vector):
+            wg = wgp.tile([P, H, 4], BF16, name="wg", tag="wg", align_bytes=64)
+            wg32 = wg[:].rearrange("p n t -> p (n t)").bitcast(F32).rearrange("p (n u) -> p n u", u=2)
+            for hh in range(2):
+                src = wps[k][hh][:].rearrange("p u n -> p n u")
+                if hh == 1 and second_on_vector:
+                    nc.vector.tensor_copy(out=wg32[:, 256 * hh:256 * hh + 256, :], in_=src)
+                else:
+                    nc.scalar.copy(out=wg32[:, 256 * hh:256 * hh + 256, :], in_=src)
+            wgs[k] = wg
+
+        def w_quantise(k):
+            nc.vector.quantize_mx(out=WC[:, k, :].bitcast(FP8X4), scales=WS[:, k, :], in_=wgs[k][:].rearrange("p n t -> p (n t)"))
+
+        xgs, xcs, zs, zbs, gs, ns, nTs, sts, mvs, nms, rss, mps = {}, {}, {}, {}, {}, {}, {}, {}, {}, {}, {}, {}
+
+        def x_regroup(s):
+            xg = xgp.tile([P, H, 4], BF16, name="xg", align_bytes=64)
+            nc.vector.tensor_copy(
+                out=xg[:].rearrange("p (b k) j -> p b k j", k=D),
+                in_=XR[:, 32 * s:32 * s + 32, :, :].rearrange("p b j k -> p b k j"),
+            )
+            xgs[s] = xg
+
+        def x_quantise(s):
+            xc = xgp.tile([P, H], U32, name="xc", align_bytes=64)
+            xs = xgp.tile([P, H], U8, name="xs", align_bytes=64)
+            nc.vector.quantize_mx(out=xc[:].bitcast(FP8X4), scales=xs[:], in_=xgs[s][:].rearrange("p c j -> p (c j)"))
+            xcs[s] = (xc, xs)
+
+        def mx1(s, r):
+            xc, xs = xcs[s]
+            z = psum.tile([P, H], F32, name="z", tag="z", bufs=2)
+            nc.tensor.matmul_mx(
+                out=z[:], lhsT=xc[:, P * r:P * r + P].bitcast(FP8X4), lhsT_scale=xs[:, P * r:P * r + P],
+                rhs=WpC[:].bitcast(FP8X4), rhs_scale=WpS[:], start=True, stop=True,
+            )
+            zs[(s, r)] = z
+
+        def bias_gelu(s, r):
+            zb = zbp.tile([P, H], F32, name="zb")
+            nc.vector.tensor_tensor(out=zb[:], in0=zs[(s, r)][:], in1=bpB[:], op=ALU.add)
+            g = gpl.tile([P, H], F32, name="g")
+            nc.scalar.activation(out=g[:], in_=zb[:], func=ACT.Gelu)
+            gs[(s, r)] = g
+
+        def stats(s, r):
+            if r == 0:
+                sts[s] = small.tile([P, 4, 6], F32, name="st4")
+            nc.vector.bn_stats(out=sts[s][:, r, :], in_=gs[(s, r)][:])
+
+        def stats_end(s):
+            mv = small.tile([P, 4, 2], F32, name="mv4")
+            for r in range(4):
+                nc.vector.bn_aggr(out=mv[:, r, :], in_=sts[s][:, r, :])
+            ve = small.tile([P, 4], F32, name="ve4")
+            nc.gpsimd.tensor_scalar(out=ve[:], in0=mv[:, :, 1], scalar1=EPS, scalar2=None, op0=ALU.add)
+            nm = small.tile([P, 4], F32, name="nm4")
+            nc.gpsimd.tensor_scalar(out=nm[:], in0=mv[:, :, 0], scalar1=-1.0, scalar2=None, op0=ALU.mult)
+            rs = small.tile([P, 4], F32, name="rs4")
+            nc.gpsimd.tensor_tensor(out=rs[:], in0=ve[:], in1=neghalf[:], op=ALU.pow)
+            nms[s] = nm
+            rss[s] = rs
+
+        def normalise(s, r, eng):
+            n = npl.tile([P, H], F32, name="n")
+            eng.tensor_scalar(
+                out=n[:], in0=gs[(s, r)][:], scalar1=nms[s][:, r:r + 1], scalar2=rss[s][:, r:r + 1], op0=ALU.add, op1=ALU.mult,
+            )
+            ns[(s, r)] = n
+
+        def n_transposes(s, r):
+            if r == 0:
+                nTs[s] = [psum.tile([P, H], F32, name="nT%d" % t, tag="nT%d" % t) for t in range(4)]
+            for t in range(4):
+                nc.tensor.transpose(out=nTs[s][t][:, P * r:P * r + P], in_=ns[(s, r)][:, P * t:P * t + P], identity=identF[:])
+
+        def affine(s, t, on_vector):
+            if t == 0:
+                mps[s] = mpp.tile([P, 4, D, 32], BF16, name="mp")
+            src = nTs[s][t][:].rearrange("p (rb k) -> p k rb", k=D)
+            if on_vector:
+                nc.vector.tensor_scalar(
+                    out=mps[s][:, t, :, :], in0=src, scalar1=GB[:, t:t + 1], scalar2=GB[:, 4 + t:5 + t], op0=ALU.mult, op1=ALU.add,
+                )
+            else:
+                nc.scalar.activation(
+                    out=mps[s][:, t, :, :], in_=src, func=ACT.Identity, scale=GB[:, t:t + 1], bias=GB[:, 4 + t:5 + t],
+                )
+
+        MGs, MCs = {}, {}
+
+        def m_regroup(s, k0, k1):
+            bh, sl = divmod(s, 4)
+            if sl == 0 and k0 == 0:
+                MGs[bh] = keep.tile([P, D, P, 4], BF16, name="MG", tag="MG", align_bytes=64)
+            nc.vector.tensor_copy(
+                out=MGs[bh][:, k0:k1, 32 * sl:32 * sl + 32, :], in_=mps[s][:, :, k0:k1, :].rearrange("p t k b -> p k b t"),
+            )
+
+        def m_quantise(bh, kg):
+            if kg == 0:
+                MC = keep.tile([P, D, P], U32, name="MC", tag="MC", align_bytes=64)
+                MS = keep.tile([P, D, P], U8, name="MS", tag="MS", align_bytes=64)
+                MCs[bh] = (MC, MS)
+            MC, MS = MCs[bh]
+            nc.vector.quantize_mx(
+                out=MC[:, 4 * kg:4 * kg + 4, :].rearrange("p k b -> p (k b)").bitcast(FP8X4),
+                scales=MS[:, 4 * kg:4 * kg + 4, :].rearrange("p k b -> p (k b)"),
+                in_=MGs[bh][:, 4 * kg:4 * kg + 4, :, :].rearrange("p k b t -> p (k b t)"),
+            )
+
+        accs, fin = {}, {}
+
+        def mx2(bh, k0, k1):
+            if k0 == 0:
+                accs[bh] = psum.tile([P, H], F32, name="acc", tag="z", bufs=2)
+            MC, MS = MCs[bh]
+            for k in range(k0, k1):
+                nc.tensor.matmul_mx(
+                    out=accs[bh][:], lhsT=MC[:, k, :].bitcast(FP8X4), lhsT_scale=MS[:, k, :],
+                    rhs=WC[:, k, :].bitcast(FP8X4), rhs_scale=WS[:, k, :], start=(k == 0), stop=(k == D - 1),
+                )
+
+        def fin_gelu(bh):
+            z2 = zbp.tile([P, H], F32, name="z2", tag="zb")
+            nc.vector.tensor_tensor(out=z2[:], in0=accs[bh][:], in1=Rsb[:, bh, :], op=ALU.add)
+            g2 = gpl.tile([P, H], F32, name="g2", tag="g")
+            nc.scalar.activation(out=g2[:], in_=z2[:], func=ACT.Gelu)
+            fin[bh] = g2
+
+        def fin_stats(bh):
+            st = small.tile([P, 6], F32, name="stf")
+            nc.vector.bn_stats(out=st[:], in_=fin[bh][:])
+            mv = small.tile([P, 2], F32, name="mvf")
+            nc.vector.bn_aggr(out=mv[:], in_=st[:])
+            ve = small.tile([P, 1], F32, name="vef")
+            nc.gpsimd.tensor_scalar(out=ve[:], in0=mv[:, 1:2], scalar1=EPS, scalar2=None, op0=ALU.add)
+            rs = small.tile([P, 1], F32, name="rsf")
+            nc.gpsimd.tensor_tensor(out=rs[:], in0=ve[:], in1=neghalf[:, 0:1], op=ALU.pow)
+            o1 = npl.tile([P, H], F32, name="o1", tag="n")
+            nc.vector.scalar_tensor_tensor(out=o1[:], in0=fin[bh][:], scalar=mv[:, 0:1], in1=gfB[:], op0=ALU.subtract, op1=ALU.mult)
+            fin[bh] = (o1, rs)
+
+        def fin_store(bh):
+            o1, rs = fin[bh]
+            o2 = zbp.tile([P, H], F32, name="o2", tag="zb")
+            nc.vector.scalar_tensor_tensor(out=o2[:], in0=o1[:], scalar=rs[:], in1=betafB[:], op0=ALU.mult, op1=ALU.add)
+            nc.sync.dma_start(out=out[P * bh:P * bh + P, :], in_=o2[:])
+
+        w_transposes(0)
+        w_copies(0, True)
+        w_transposes(1)
+        w_copies(1, True)
+        x_regroup(0)
+        w_quantise(0)
+        x_quantise(0)
+        spread_bp()
+        w_quantise(1)
+        next_w = 2
+        pend = None
+        for i in range(NS):
+            j = i - 1
+            late_loads(i)
+            wa, wb = None, None
+            if next_w < D:
+                wa, wb = next_w, next_w + 1
+                next_w += 2
+            if pend is not None:
+                w_copies(pend, False)
+            if j >= 0:
+                for r in range(4):
+                    normalise(j, r, nc.gpsimd)
+            mx1(i, 0)
+            mx1(i, 1)
+            bias_gelu(i, 0)
+            bias_gelu(i, 1)
+            mx1(i, 2)
+            mx1(i, 3)
+            if j >= 0:
+                n_transposes(j, 0)
+                n_transposes(j, 1)
+            if wa is not None:
+                w_transposes(wa)
+            if pend is not None:
+                w_quantise(pend)
+            bias_gelu(i, 2)
+            bias_gelu(i, 3)
+            if j >= 0:
+                n_transposes(j, 2)
+                n_transposes(j, 3)
+            if wa is not None:
+                w_copies(wa, False)
+            if wb is not None:
+                w_transposes(wb)
+            if i == NS - 1:
+                mx2(0, 0, 8)
+            if i == 0:
+                spread_rest()
+            if i + 1 < NS:
+                x_regroup(i + 1)
+            stats(i, 0)
+            stats(i, 1)
+            if i + 1 < NS:
+                x_quantise(i + 1)
+            stats(i, 2)
+            if wa is not None:
+                w_quantise(wa)
+            stats(i, 3)
+            stats_end(i)
+            if j >= 0:
+                for t in range(4):
+                    affine(j, t, False)
+                if i < NS - 1:
+                    m_regroup(j, 0, D)
+            if j == 3:
+                for kg in range(4):
+                    m_quantise(0, kg)
+            pend = wb
+
+        last = NS - 1
+        for r in range(4):
+            normalise(last, r, nc.vector)
+            n_transposes(last, r)
+        mx2(0, 8, D)
+        m_regroup(last - 1, 0, D)
+        affine(last, 0, False)
+        affine(last, 1, False)
+        affine(last, 2, True)
+        affine(last, 3, True)
+        m_regroup(last, 0, 8)
+        m_regroup(last, 8, D)
+        for kg in range(4):
+            m_quantise(1, kg)
+            mx2(1, 4 * kg, 4 * kg + 4)
+        fin_gelu(0)
+        fin_stats(0)
+        fin_gelu(1)
+        fin_store(0)
+        fin_stats(1)
+        fin_store(1)

@@ -100,7 +100,6 @@ def tile_conduitdecoder_pa_kernel(
                 in_=Wp[256 * u:256 * u + 256, :].rearrange("(p e) i -> p e i", e=2),
             )
         load_u(0)
-        load_wf(0)
         for (pp, j, vec) in ((122, 3, S), (127, 1, settle), (127, 2, char_coeffs), (127, 3, ext_order)):
             nc.gpsimd.dma_start(out=XR[pp:pp + 1, :, j, :], in_=vec.rearrange("(o b) k -> o b k", o=1))
         nc.gpsimd.dma_start(out=VEC[0:1, 0, :], in_=bp.rearrange("(o n) -> o n", o=1))
@@ -130,9 +129,10 @@ def tile_conduitdecoder_pa_kernel(
         )
         load_u_high(0)
         load_vt(0, 64)
+        load_wf(0)
         load_u(1)
-        load_wf(1)
         load_vt(64, 256)
+        load_wf(1)
         load_u(2)
         load_u_high(1)
         load_wf(2)
@@ -274,14 +274,22 @@ def tile_conduitdecoder_pa_kernel(
             nc.gpsimd.tensor_scalar(out=nm[:], in0=mv[:, :, 0], scalar1=-1.0, scalar2=None, op0=ALU.mult)
             rs = small.tile([P, 4], F32, name="rs4")
             nc.gpsimd.tensor_tensor(out=rs[:], in0=ve[:], in1=neghalf[:], op=ALU.pow)
-            nms[s] = nm
+            nb = small.tile([P, 4], F32, name="nb4")
+            nc.gpsimd.tensor_tensor(out=nb[:], in0=nm[:], in1=rs[:], op=ALU.mult)
+            nms[s] = nb
             rss[s] = rs
 
         def normalise(s, r, eng):
             n = npl.tile([P, H], F32, name="n")
-            eng.tensor_scalar(
-                out=n[:], in0=gs[(s, r)][:], scalar1=nms[s][:, r:r + 1], scalar2=rss[s][:, r:r + 1], op0=ALU.add, op1=ALU.mult,
-            )
+            if eng == "scalar":
+                nc.scalar.activation(
+                    out=n[:], in_=gs[(s, r)][:], func=ACT.Identity, scale=rss[s][:, r:r + 1], bias=nms[s][:, r:r + 1],
+                )
+            else:
+                engine = nc.gpsimd if eng == "gpsimd" else nc.vector
+                engine.tensor_scalar(
+                    out=n[:], in0=gs[(s, r)][:], scalar1=rss[s][:, r:r + 1], scalar2=nms[s][:, r:r + 1], op0=ALU.mult, op1=ALU.add,
+                )
             ns[(s, r)] = n
 
         def n_transposes(s, r):
@@ -363,53 +371,47 @@ def tile_conduitdecoder_pa_kernel(
             nc.vector.scalar_tensor_tensor(out=o2[:], in0=o1[:], scalar=rs[:], in1=betafB[:], op0=ALU.mult, op1=ALU.add)
             nc.sync.dma_start(out=out[P * bh:P * bh + P, :], in_=o2[:])
 
-        w_transposes(0)
-        w_copies(0, True)
-        w_transposes(1)
-        w_copies(1, True)
         x_regroup(0)
-        w_quantise(0)
-        x_quantise(0)
         spread_bp()
-        w_quantise(1)
-        next_w = 2
-        pend = None
+        x_quantise(0)
+        next_w = 0
+        p = None
         for i in range(NS):
             j = i - 1
-            late_loads(i)
-            wa, wb = None, None
-            if next_w < D:
-                wa, wb = next_w, next_w + 1
-                next_w += 2
-            if pend is not None:
-                w_copies(pend, False)
+            q = next_w
+            next_w += 1
+            if p is not None:
+                w_copies(p, False)
             if j >= 0:
-                for r in range(4):
-                    normalise(j, r, nc.gpsimd)
+                normalise(j, 3, "gpsimd")
             mx1(i, 0)
             mx1(i, 1)
             bias_gelu(i, 0)
             bias_gelu(i, 1)
             mx1(i, 2)
             mx1(i, 3)
+            w_transposes(q)
+            if j >= 1:
+                m_regroup(j - 1, 0, D)
+            if j - 1 == 3:
+                m_quantise(0, 0)
+                m_quantise(0, 1)
+            if p is not None:
+                w_quantise(p)
             if j >= 0:
-                n_transposes(j, 0)
-                n_transposes(j, 1)
-            if wa is not None:
-                w_transposes(wa)
-            if pend is not None:
-                w_quantise(pend)
+                for r in range(3):
+                    normalise(j, r, "scalar")
+                    n_transposes(j, r)
+                n_transposes(j, 3)
             bias_gelu(i, 2)
             bias_gelu(i, 3)
-            if j >= 0:
-                n_transposes(j, 2)
-                n_transposes(j, 3)
-            if wa is not None:
-                w_copies(wa, False)
-            if wb is not None:
-                w_transposes(wb)
+            w_copies(q, False)
+            p = next_w
+            next_w += 1
+            w_transposes(p)
+            late_loads(i)
             if i == NS - 1:
-                mx2(0, 0, 8)
+                mx2(0, 0, 14)
             if i == 0:
                 spread_rest()
             if i + 1 < NS:
@@ -419,26 +421,24 @@ def tile_conduitdecoder_pa_kernel(
             if i + 1 < NS:
                 x_quantise(i + 1)
             stats(i, 2)
-            if wa is not None:
-                w_quantise(wa)
+            w_quantise(q)
             stats(i, 3)
             stats_end(i)
+            if j - 1 == 3:
+                m_quantise(0, 2)
+                m_quantise(0, 3)
             if j >= 0:
                 for t in range(4):
                     affine(j, t, False)
-                if i < NS - 1:
-                    m_regroup(j, 0, D)
-            if j == 3:
-                for kg in range(4):
-                    m_quantise(0, kg)
-            pend = wb
 
         last = NS - 1
-        for r in range(4):
-            normalise(last, r, nc.vector)
-            n_transposes(last, r)
-        mx2(0, 8, D)
+        w_copies(p, False)
         m_regroup(last - 1, 0, D)
+        for r in range(4):
+            normalise(last, r, "vector")
+            n_transposes(last, r)
+        w_quantise(p)
+        mx2(0, 14, D)
         affine(last, 0, False)
         affine(last, 1, False)
         affine(last, 2, True)

@@ -37,6 +37,7 @@ def tile_conduitdecoder_pa_kernel(
         npl = ctx.enter_context(tc.tile_pool(name="npl", bufs=4))
         mpp = ctx.enter_context(tc.tile_pool(name="mpp", bufs=2))
         small = ctx.enter_context(tc.tile_pool(name="small", bufs=2))
+        junkp = ctx.enter_context(tc.tile_pool(name="junkp", bufs=1))
         psum = ctx.enter_context(tc.psum_pool(name="psum", bufs=1))
 
         identF = const.tile([P, P], F32, name="identF")
@@ -227,13 +228,13 @@ def tile_conduitdecoder_pa_kernel(
         def w_quantise(k):
             nc.vector.quantize_mx(out=WC[:, k, :].bitcast(FP8X4), scales=WS[:, k, :], in_=wgs[k][:].rearrange("p n t -> p (n t)"))
 
-        xgs, xcs, zs, zbs, gs, ns, nTs, sts, mvs, nms, rss, mps = {}, {}, {}, {}, {}, {}, {}, {}, {}, {}, {}, {}
+        xgs, xcs, zs, gs, ns, nTs, sts, nms, nbs, rss, mps = {}, {}, {}, {}, {}, {}, {}, {}, {}, {}, {}
 
         def x_regroup(s):
             xg = xgp.tile([P, H, 4], BF16, name="xg", align_bytes=64)
             nc.vector.tensor_copy(
-                out=xg[:].rearrange("p (b k) j -> p b k j", k=D),
-                in_=XR[:, 32 * s:32 * s + 32, :, :].rearrange("p b j k -> p b k j"),
+                out=xg[:].rearrange("p (b c i) j -> p b c j i", c=4, i=4),
+                in_=XR[:, 32 * s:32 * s + 32, :, :].rearrange("p b j (c i) -> p b c j i", i=4),
             )
             xgs[s] = xg
 
@@ -252,43 +253,59 @@ def tile_conduitdecoder_pa_kernel(
             )
             zs[(s, r)] = z
 
+        sgs, sss = {}, {}
+
         def bias_gelu(s, r):
             zb = zbp.tile([P, H], F32, name="zb")
             nc.vector.tensor_tensor(out=zb[:], in0=zs[(s, r)][:], in1=bpB[:], op=ALU.add)
             g = gpl.tile([P, H], F32, name="g")
-            nc.scalar.activation(out=g[:], in_=zb[:], func=ACT.Gelu)
+            if r == 3:
+                sgs[s] = small.tile([P, 1], F32, name="sg")
+                nc.scalar.activation(out=g[:], in_=zb[:], func=ACT.Gelu, accum_out=sgs[s][:])
+                nms[s] = small.tile([P, 4], F32, name="nm4")
+                nc.gpsimd.tensor_scalar(out=nms[s][:, 3:4], in0=sgs[s][:], scalar1=-1.0 / H, scalar2=None, op0=ALU.mult)
+            else:
+                nc.scalar.activation(out=g[:], in_=zb[:], func=ACT.Gelu)
             gs[(s, r)] = g
+
+        def square_sum(s):
+            junk = junkp.tile([P, H], BF16, name="junk")
+            sss[s] = small.tile([P, 1], F32, name="ss")
+            nc.scalar.activation(
+                out=junk[:], in_=gs[(s, 3)][:], func=ACT.Square, bias=nms[s][:, 3:4], scale=1.0, accum_out=sss[s][:],
+            )
 
         def stats(s, r):
             if r == 0:
-                sts[s] = small.tile([P, 4, 6], F32, name="st4")
+                sts[s] = small.tile([P, 3, 6], F32, name="st4")
             nc.vector.bn_stats(out=sts[s][:, r, :], in_=gs[(s, r)][:])
 
         def stats_end(s):
-            mv = small.tile([P, 4, 2], F32, name="mv4")
-            for r in range(4):
+            mv = small.tile([P, 3, 2], F32, name="mv4")
+            for r in range(3):
                 nc.vector.bn_aggr(out=mv[:, r, :], in_=sts[s][:, r, :])
+            nm = nms[s]
             ve = small.tile([P, 4], F32, name="ve4")
-            nc.gpsimd.tensor_scalar(out=ve[:], in0=mv[:, :, 1], scalar1=EPS, scalar2=None, op0=ALU.add)
-            nm = small.tile([P, 4], F32, name="nm4")
-            nc.gpsimd.tensor_scalar(out=nm[:], in0=mv[:, :, 0], scalar1=-1.0, scalar2=None, op0=ALU.mult)
+            nc.gpsimd.tensor_scalar(out=ve[:, 0:3], in0=mv[:, :, 1], scalar1=EPS, scalar2=None, op0=ALU.add)
+            nc.gpsimd.tensor_scalar(out=ve[:, 3:4], in0=sss[s][:], scalar1=1.0 / H, scalar2=EPS, op0=ALU.mult, op1=ALU.add)
+            nc.gpsimd.tensor_scalar(out=nm[:, 0:3], in0=mv[:, :, 0], scalar1=-1.0, scalar2=None, op0=ALU.mult)
             rs = small.tile([P, 4], F32, name="rs4")
             nc.gpsimd.tensor_tensor(out=rs[:], in0=ve[:], in1=neghalf[:], op=ALU.pow)
             nb = small.tile([P, 4], F32, name="nb4")
             nc.gpsimd.tensor_tensor(out=nb[:], in0=nm[:], in1=rs[:], op=ALU.mult)
-            nms[s] = nb
+            nbs[s] = nb
             rss[s] = rs
 
         def normalise(s, r, eng):
             n = npl.tile([P, H], F32, name="n")
             if eng == "scalar":
                 nc.scalar.activation(
-                    out=n[:], in_=gs[(s, r)][:], func=ACT.Identity, scale=rss[s][:, r:r + 1], bias=nms[s][:, r:r + 1],
+                    out=n[:], in_=gs[(s, r)][:], func=ACT.Identity, scale=rss[s][:, r:r + 1], bias=nbs[s][:, r:r + 1],
                 )
             else:
                 engine = nc.gpsimd if eng == "gpsimd" else nc.vector
                 engine.tensor_scalar(
-                    out=n[:], in0=gs[(s, r)][:], scalar1=rss[s][:, r:r + 1], scalar2=nms[s][:, r:r + 1], op0=ALU.mult, op1=ALU.add,
+                    out=n[:], in0=gs[(s, r)][:], scalar1=rss[s][:, r:r + 1], scalar2=nbs[s][:, r:r + 1], op0=ALU.mult, op1=ALU.add,
                 )
             ns[(s, r)] = n
 
@@ -318,7 +335,8 @@ def tile_conduitdecoder_pa_kernel(
             if sl == 0 and k0 == 0:
                 MGs[bh] = keep.tile([P, D, P, 4], BF16, name="MG", tag="MG", align_bytes=64)
             nc.vector.tensor_copy(
-                out=MGs[bh][:, k0:k1, 32 * sl:32 * sl + 32, :], in_=mps[s][:, :, k0:k1, :].rearrange("p t k b -> p k b t"),
+                out=MGs[bh][:, k0:k1, 32 * sl:32 * sl + 32, :].rearrange("p k (c i) t -> p k c t i", i=4),
+                in_=mps[s][:, :, k0:k1, :].rearrange("p t k (c i) -> p k c t i", i=4),
             )
 
         def m_quantise(bh, kg):
@@ -406,6 +424,7 @@ def tile_conduitdecoder_pa_kernel(
             bias_gelu(i, 2)
             bias_gelu(i, 3)
             w_copies(q, False)
+            square_sum(i)
             p = next_w
             next_w += 1
             w_transposes(p)
@@ -422,7 +441,6 @@ def tile_conduitdecoder_pa_kernel(
                 x_quantise(i + 1)
             stats(i, 2)
             w_quantise(q)
-            stats(i, 3)
             stats_end(i)
             if j - 1 == 3:
                 m_quantise(0, 2)

@@ -228,7 +228,7 @@ def tile_conduitdecoder_pa_kernel(
         def w_quantise(k):
             nc.vector.quantize_mx(out=WC[:, k, :].bitcast(FP8X4), scales=WS[:, k, :], in_=wgs[k][:].rearrange("p n t -> p (n t)"))
 
-        xgs, xcs, zs, gs, ns, nTs, sts, nms, nbs, rss, mps = {}, {}, {}, {}, {}, {}, {}, {}, {}, {}, {}
+        xgs, xcs, zs, zbs, gs, ns, nTs, sts, nbs, rss, mps = {}, {}, {}, {}, {}, {}, {}, {}, {}, {}, {}
 
         def x_regroup(s):
             xg = xgp.tile([P, H, 4], BF16, name="xg", align_bytes=64)
@@ -253,26 +253,35 @@ def tile_conduitdecoder_pa_kernel(
             )
             zs[(s, r)] = z
 
-        sgs, sss = {}, {}
+        sgs, sss, mvs = {}, {}, {}
 
-        def bias_gelu(s, r):
+        def bias_add(s, r):
             zb = zbp.tile([P, H], F32, name="zb")
             nc.vector.tensor_tensor(out=zb[:], in0=zs[(s, r)][:], in1=bpB[:], op=ALU.add)
+            zbs[(s, r)] = zb
+
+        def gelu(s, r):
             g = gpl.tile([P, H], F32, name="g")
             if r == 3:
                 sgs[s] = small.tile([P, 1], F32, name="sg")
-                nc.scalar.activation(out=g[:], in_=zb[:], func=ACT.Gelu, accum_out=sgs[s][:])
-                nms[s] = small.tile([P, 4], F32, name="nm4")
-                nc.gpsimd.tensor_scalar(out=nms[s][:, 3:4], in0=sgs[s][:], scalar1=-1.0 / H, scalar2=None, op0=ALU.mult)
+                nc.scalar.activation(out=g[:], in_=zbs[(s, r)][:], func=ACT.Gelu, accum_out=sgs[s][:])
             else:
-                nc.scalar.activation(out=g[:], in_=zb[:], func=ACT.Gelu)
+                nc.scalar.activation(out=g[:], in_=zbs[(s, r)][:], func=ACT.Gelu)
             gs[(s, r)] = g
+
+        def bias_gelu(s, r):
+            bias_add(s, r)
+            gelu(s, r)
+
+        def mean3(s):
+            mvs[s] = small.tile([P, 4, 2], F32, name="mv4")
+            nc.vector.tensor_scalar(out=mvs[s][:, 3, 0:1], in0=sgs[s][:], scalar1=1.0 / H, scalar2=None, op0=ALU.mult)
 
         def square_sum(s):
             junk = junkp.tile([P, H], BF16, name="junk")
             sss[s] = small.tile([P, 1], F32, name="ss")
             nc.scalar.activation(
-                out=junk[:], in_=gs[(s, 3)][:], func=ACT.Square, bias=nms[s][:, 3:4], scale=1.0, accum_out=sss[s][:],
+                out=junk[:], in_=gs[(s, 3)][:], func=ACT.Square, bias=mvs[s][:, 3, 0:1], scale=-1.0, accum_out=sss[s][:],
             )
 
         def stats(s, r):
@@ -281,20 +290,20 @@ def tile_conduitdecoder_pa_kernel(
             nc.vector.bn_stats(out=sts[s][:, r, :], in_=gs[(s, r)][:])
 
         def stats_end(s):
-            mv = small.tile([P, 3, 2], F32, name="mv4")
+            mv = mvs[s]
             for r in range(3):
                 nc.vector.bn_aggr(out=mv[:, r, :], in_=sts[s][:, r, :])
-            nm = nms[s]
             ve = small.tile([P, 4], F32, name="ve4")
-            nc.gpsimd.tensor_scalar(out=ve[:, 0:3], in0=mv[:, :, 1], scalar1=EPS, scalar2=None, op0=ALU.add)
-            nc.gpsimd.tensor_scalar(out=ve[:, 3:4], in0=sss[s][:], scalar1=1.0 / H, scalar2=EPS, op0=ALU.mult, op1=ALU.add)
-            nc.gpsimd.tensor_scalar(out=nm[:, 0:3], in0=mv[:, :, 0], scalar1=-1.0, scalar2=None, op0=ALU.mult)
+            nc.vector.tensor_scalar(out=ve[:, 0:3], in0=mv[:, 0:3, 1], scalar1=EPS, scalar2=None, op0=ALU.add)
+            nc.vector.tensor_scalar(out=ve[:, 3:4], in0=sss[s][:], scalar1=1.0 / H, scalar2=EPS, op0=ALU.mult, op1=ALU.add)
             rs = small.tile([P, 4], F32, name="rs4")
             nc.gpsimd.tensor_tensor(out=rs[:], in0=ve[:], in1=neghalf[:], op=ALU.pow)
-            nb = small.tile([P, 4], F32, name="nb4")
-            nc.gpsimd.tensor_tensor(out=nb[:], in0=nm[:], in1=rs[:], op=ALU.mult)
-            nbs[s] = nb
             rss[s] = rs
+
+        def shift(s):
+            nb = small.tile([P, 4], F32, name="nb4")
+            nc.vector.scalar_tensor_tensor(out=nb[:], in0=mvs[s][:, :, 0], scalar=-1.0, in1=rss[s][:], op0=ALU.mult, op1=ALU.mult)
+            nbs[s] = nb
 
         def normalise(s, r, eng):
             n = npl.tile([P, H], F32, name="n")
@@ -376,7 +385,7 @@ def tile_conduitdecoder_pa_kernel(
             mv = small.tile([P, 2], F32, name="mvf")
             nc.vector.bn_aggr(out=mv[:], in_=st[:])
             ve = small.tile([P, 1], F32, name="vef")
-            nc.gpsimd.tensor_scalar(out=ve[:], in0=mv[:, 1:2], scalar1=EPS, scalar2=None, op0=ALU.add)
+            nc.vector.tensor_scalar(out=ve[:], in0=mv[:, 1:2], scalar1=EPS, scalar2=None, op0=ALU.add)
             rs = small.tile([P, 1], F32, name="rsf")
             nc.gpsimd.tensor_tensor(out=rs[:], in0=ve[:], in1=neghalf[:, 0:1], op=ALU.pow)
             o1 = npl.tile([P, H], F32, name="o1", tag="n")
@@ -392,6 +401,8 @@ def tile_conduitdecoder_pa_kernel(
         x_regroup(0)
         spread_bp()
         x_quantise(0)
+        mx1(0, 0)
+        mx1(0, 1)
         next_w = 0
         p = None
         for i in range(NS):
@@ -400,10 +411,6 @@ def tile_conduitdecoder_pa_kernel(
             next_w += 1
             if p is not None:
                 w_copies(p, False)
-            if j >= 0:
-                normalise(j, 3, "gpsimd")
-            mx1(i, 0)
-            mx1(i, 1)
             bias_gelu(i, 0)
             bias_gelu(i, 1)
             mx1(i, 2)
@@ -417,14 +424,26 @@ def tile_conduitdecoder_pa_kernel(
             if p is not None:
                 w_quantise(p)
             if j >= 0:
+                shift(j)
+                normalise(j, 3, "gpsimd")
+            bias_gelu(i, 2)
+            bias_gelu(i, 3)
+            if j >= 0:
                 for r in range(3):
                     normalise(j, r, "scalar")
                     n_transposes(j, r)
                 n_transposes(j, 3)
-            bias_gelu(i, 2)
-            bias_gelu(i, 3)
-            w_copies(q, False)
+            if i + 1 < NS:
+                x_regroup(i + 1)
+            mean3(i)
             square_sum(i)
+            w_copies(q, False)
+            stats(i, 0)
+            stats(i, 1)
+            if i + 1 < NS:
+                x_quantise(i + 1)
+                mx1(i + 1, 0)
+                mx1(i + 1, 1)
             p = next_w
             next_w += 1
             w_transposes(p)
@@ -433,12 +452,6 @@ def tile_conduitdecoder_pa_kernel(
                 mx2(0, 0, 14)
             if i == 0:
                 spread_rest()
-            if i + 1 < NS:
-                x_regroup(i + 1)
-            stats(i, 0)
-            stats(i, 1)
-            if i + 1 < NS:
-                x_quantise(i + 1)
             stats(i, 2)
             w_quantise(q)
             stats_end(i)
@@ -452,6 +465,7 @@ def tile_conduitdecoder_pa_kernel(
         last = NS - 1
         w_copies(p, False)
         m_regroup(last - 1, 0, D)
+        shift(last)
         for r in range(4):
             normalise(last, r, "vector")
             n_transposes(last, r)
@@ -462,8 +476,10 @@ def tile_conduitdecoder_pa_kernel(
         affine(last, 2, True)
         affine(last, 3, True)
         m_regroup(last, 0, 8)
+        m_quantise(1, 0)
+        mx2(1, 0, 4)
         m_regroup(last, 8, D)
-        for kg in range(4):
+        for kg in range(1, 4):
             m_quantise(1, kg)
             mx2(1, 4 * kg, 4 * kg + 4)
         fin_gelu(0)

@@ -29,7 +29,7 @@ def tile_conduitdecoder_pa_kernel(
         const = ctx.enter_context(tc.tile_pool(name="const", bufs=1))
         keep = ctx.enter_context(tc.tile_pool(name="keep", bufs=1))
         setup = ctx.enter_context(tc.tile_pool(name="setup", bufs=1))
-        wrp = ctx.enter_context(tc.tile_pool(name="wrp", bufs=4))
+        wrp = ctx.enter_context(tc.tile_pool(name="wrp", bufs=3))
         wgp = ctx.enter_context(tc.tile_pool(name="wgp", bufs=3))
         xgp = ctx.enter_context(tc.tile_pool(name="xgp", bufs=2))
         zbp = ctx.enter_context(tc.tile_pool(name="zbp", bufs=3))
@@ -130,22 +130,20 @@ def tile_conduitdecoder_pa_kernel(
         )
         load_u_high(0)
         load_vt(0, 64)
-        load_wf(0)
         load_u(1)
         load_vt(64, 256)
-        load_wf(1)
         load_u(2)
         load_u_high(1)
-        load_wf(2)
         load_u(3)
-        load_wf(3)
-
-        def late_loads(i):
-            if i < 4:
-                load_u(4 + i)
-                if i % 2 == 0:
-                    load_u_high(2 + i // 2)
-                load_wf(4 + i)
+        load_u(4)
+        load_u_high(2)
+        load_u(5)
+        load_u(6)
+        load_u_high(3)
+        load_u(7)
+        load_wf(0)
+        load_wf(1)
+        load_wf(2)
 
         WpC = const.tile([P, H], U32, name="WpC", align_bytes=64)
         WpS = const.tile([P, H], U8, name="WpS", align_bytes=64)
@@ -213,8 +211,10 @@ def tile_conduitdecoder_pa_kernel(
                         nc.tensor.transpose(out=pt[:, u, P * a:P * a + P], in_=wr32[:, 2 * hh + a, w0:w0 + P], identity=identF[:])
                 tiles.append(pt)
             wps[k] = tiles
+            if half == 1 and c + 3 < 8:
+                load_wf(c + 3)
 
-        def w_copies(k, second_on_vector):
+        def w_copies(k, second_on_vector=False):
             wg = wgp.tile([P, H, 4], BF16, name="wg", tag="wg", align_bytes=64)
             wg32 = wg[:].rearrange("p n t -> p (n t)").bitcast(F32).rearrange("p (n u) -> p n u", u=2)
             for hh in range(2):
@@ -228,7 +228,7 @@ def tile_conduitdecoder_pa_kernel(
         def w_quantise(k):
             nc.vector.quantize_mx(out=WC[:, k, :].bitcast(FP8X4), scales=WS[:, k, :], in_=wgs[k][:].rearrange("p n t -> p (n t)"))
 
-        xgs, xcs, zs, zbs, gs, ns, nTs, sts, nbs, rss, mps = {}, {}, {}, {}, {}, {}, {}, {}, {}, {}, {}
+        xgs, xcs, zs, gs, ns, nTs, sts, nms, nbs, rss, mps = {}, {}, {}, {}, {}, {}, {}, {}, {}, {}, {}
 
         def x_regroup(s):
             xg = xgp.tile([P, H, 4], BF16, name="xg", align_bytes=64)
@@ -253,35 +253,26 @@ def tile_conduitdecoder_pa_kernel(
             )
             zs[(s, r)] = z
 
-        sgs, sss, mvs = {}, {}, {}
+        sgs, sss = {}, {}
 
-        def bias_add(s, r):
+        def bias_gelu(s, r):
             zb = zbp.tile([P, H], F32, name="zb")
             nc.vector.tensor_tensor(out=zb[:], in0=zs[(s, r)][:], in1=bpB[:], op=ALU.add)
-            zbs[(s, r)] = zb
-
-        def gelu(s, r):
             g = gpl.tile([P, H], F32, name="g")
             if r == 3:
                 sgs[s] = small.tile([P, 1], F32, name="sg")
-                nc.scalar.activation(out=g[:], in_=zbs[(s, r)][:], func=ACT.Gelu, accum_out=sgs[s][:])
+                nc.scalar.activation(out=g[:], in_=zb[:], func=ACT.Gelu, accum_out=sgs[s][:])
+                nms[s] = small.tile([P, 4], F32, name="nm4")
+                nc.gpsimd.tensor_scalar(out=nms[s][:, 3:4], in0=sgs[s][:], scalar1=-1.0 / H, scalar2=None, op0=ALU.mult)
             else:
-                nc.scalar.activation(out=g[:], in_=zbs[(s, r)][:], func=ACT.Gelu)
+                nc.scalar.activation(out=g[:], in_=zb[:], func=ACT.Gelu)
             gs[(s, r)] = g
-
-        def bias_gelu(s, r):
-            bias_add(s, r)
-            gelu(s, r)
-
-        def mean3(s):
-            mvs[s] = small.tile([P, 4, 2], F32, name="mv4")
-            nc.vector.tensor_scalar(out=mvs[s][:, 3, 0:1], in0=sgs[s][:], scalar1=1.0 / H, scalar2=None, op0=ALU.mult)
 
         def square_sum(s):
             junk = junkp.tile([P, H], BF16, name="junk")
             sss[s] = small.tile([P, 1], F32, name="ss")
             nc.scalar.activation(
-                out=junk[:], in_=gs[(s, 3)][:], func=ACT.Square, bias=mvs[s][:, 3, 0:1], scale=-1.0, accum_out=sss[s][:],
+                out=junk[:], in_=gs[(s, 3)][:], func=ACT.Square, bias=nms[s][:, 3:4], scale=1.0, accum_out=sss[s][:],
             )
 
         def stats(s, r):
@@ -290,20 +281,20 @@ def tile_conduitdecoder_pa_kernel(
             nc.vector.bn_stats(out=sts[s][:, r, :], in_=gs[(s, r)][:])
 
         def stats_end(s):
-            mv = mvs[s]
+            mv = small.tile([P, 3, 2], F32, name="mv4")
             for r in range(3):
                 nc.vector.bn_aggr(out=mv[:, r, :], in_=sts[s][:, r, :])
+            nm = nms[s]
             ve = small.tile([P, 4], F32, name="ve4")
-            nc.vector.tensor_scalar(out=ve[:, 0:3], in0=mv[:, 0:3, 1], scalar1=EPS, scalar2=None, op0=ALU.add)
-            nc.vector.tensor_scalar(out=ve[:, 3:4], in0=sss[s][:], scalar1=1.0 / H, scalar2=EPS, op0=ALU.mult, op1=ALU.add)
+            nc.gpsimd.tensor_scalar(out=ve[:, 0:3], in0=mv[:, :, 1], scalar1=EPS, scalar2=None, op0=ALU.add)
+            nc.gpsimd.tensor_scalar(out=ve[:, 3:4], in0=sss[s][:], scalar1=1.0 / H, scalar2=EPS, op0=ALU.mult, op1=ALU.add)
+            nc.gpsimd.tensor_scalar(out=nm[:, 0:3], in0=mv[:, :, 0], scalar1=-1.0, scalar2=None, op0=ALU.mult)
             rs = small.tile([P, 4], F32, name="rs4")
             nc.gpsimd.tensor_tensor(out=rs[:], in0=ve[:], in1=neghalf[:], op=ALU.pow)
-            rss[s] = rs
-
-        def shift(s):
             nb = small.tile([P, 4], F32, name="nb4")
-            nc.vector.scalar_tensor_tensor(out=nb[:], in0=mvs[s][:, :, 0], scalar=-1.0, in1=rss[s][:], op0=ALU.mult, op1=ALU.mult)
+            nc.gpsimd.tensor_tensor(out=nb[:], in0=nm[:], in1=rs[:], op=ALU.mult)
             nbs[s] = nb
+            rss[s] = rs
 
         def normalise(s, r, eng):
             n = npl.tile([P, H], F32, name="n")
@@ -350,8 +341,8 @@ def tile_conduitdecoder_pa_kernel(
 
         def m_quantise(bh, kg):
             if kg == 0:
-                MC = keep.tile([P, D, P], U32, name="MC", tag="MC", align_bytes=64)
-                MS = keep.tile([P, D, P], U8, name="MS", tag="MS", align_bytes=64)
+                MC = keep.tile([P, D, P], U32, name="MC", tag="MC", align_bytes=64, bufs=2)
+                MS = keep.tile([P, D, P], U8, name="MS", tag="MS", align_bytes=64, bufs=2)
                 MCs[bh] = (MC, MS)
             MC, MS = MCs[bh]
             nc.vector.quantize_mx(
@@ -385,7 +376,7 @@ def tile_conduitdecoder_pa_kernel(
             mv = small.tile([P, 2], F32, name="mvf")
             nc.vector.bn_aggr(out=mv[:], in_=st[:])
             ve = small.tile([P, 1], F32, name="vef")
-            nc.vector.tensor_scalar(out=ve[:], in0=mv[:, 1:2], scalar1=EPS, scalar2=None, op0=ALU.add)
+            nc.gpsimd.tensor_scalar(out=ve[:], in0=mv[:, 1:2], scalar1=EPS, scalar2=None, op0=ALU.add)
             rs = small.tile([P, 1], F32, name="rsf")
             nc.gpsimd.tensor_tensor(out=rs[:], in0=ve[:], in1=neghalf[:, 0:1], op=ALU.pow)
             o1 = npl.tile([P, H], F32, name="o1", tag="n")
@@ -401,59 +392,42 @@ def tile_conduitdecoder_pa_kernel(
         x_regroup(0)
         spread_bp()
         x_quantise(0)
-        mx1(0, 0)
-        mx1(0, 1)
-        next_w = 0
-        p = None
         for i in range(NS):
             j = i - 1
-            q = next_w
-            next_w += 1
-            if p is not None:
-                w_copies(p, False)
+            if j >= 0:
+                normalise(j, 3, "gpsimd")
+            mx1(i, 0)
+            mx1(i, 1)
             bias_gelu(i, 0)
             bias_gelu(i, 1)
             mx1(i, 2)
             mx1(i, 3)
-            w_transposes(q)
             if j >= 1:
                 m_regroup(j - 1, 0, D)
             if j - 1 == 3:
                 m_quantise(0, 0)
                 m_quantise(0, 1)
-            if p is not None:
-                w_quantise(p)
-            if j >= 0:
-                shift(j)
-                normalise(j, 3, "gpsimd")
-            bias_gelu(i, 2)
-            bias_gelu(i, 3)
             if j >= 0:
                 for r in range(3):
                     normalise(j, r, "scalar")
                     n_transposes(j, r)
                 n_transposes(j, 3)
+            bias_gelu(i, 2)
+            bias_gelu(i, 3)
+            square_sum(i)
+            if i == 0:
+                spread_rest()
+            if i == NS - 1:
+                w_transposes(0)
+                w_copies(0)
+                w_transposes(1)
             if i + 1 < NS:
                 x_regroup(i + 1)
-            mean3(i)
-            square_sum(i)
-            w_copies(q, False)
             stats(i, 0)
             stats(i, 1)
             if i + 1 < NS:
                 x_quantise(i + 1)
-                mx1(i + 1, 0)
-                mx1(i + 1, 1)
-            p = next_w
-            next_w += 1
-            w_transposes(p)
-            late_loads(i)
-            if i == NS - 1:
-                mx2(0, 0, 14)
-            if i == 0:
-                spread_rest()
             stats(i, 2)
-            w_quantise(q)
             stats_end(i)
             if j - 1 == 3:
                 m_quantise(0, 2)
@@ -463,28 +437,40 @@ def tile_conduitdecoder_pa_kernel(
                     affine(j, t, False)
 
         last = NS - 1
-        w_copies(p, False)
+        w_copies(1)
+        w_transposes(2)
         m_regroup(last - 1, 0, D)
-        shift(last)
         for r in range(4):
             normalise(last, r, "vector")
             n_transposes(last, r)
-        w_quantise(p)
-        mx2(0, 14, D)
+        w_quantise(0)
+        w_quantise(1)
+        mx2(0, 0, 2)
+        w_copies(2)
+        w_transposes(3)
         affine(last, 0, False)
         affine(last, 1, False)
         affine(last, 2, True)
         affine(last, 3, True)
+        w_copies(3)
+        w_transposes(4)
         m_regroup(last, 0, 8)
         m_quantise(1, 0)
-        mx2(1, 0, 4)
         m_regroup(last, 8, D)
         for kg in range(1, 4):
             m_quantise(1, kg)
-            mx2(1, 4 * kg, 4 * kg + 4)
+        mx2(1, 0, 2)
+        for k in range(2, D):
+            w_quantise(k)
+            mx2(0, k, k + 1)
+            mx2(1, k, k + 1)
+            if k + 2 < D:
+                w_copies(k + 2)
+            if k + 3 < D:
+                w_transposes(k + 3)
         fin_gelu(0)
-        fin_stats(0)
         fin_gelu(1)
-        fin_store(0)
+        fin_stats(0)
         fin_stats(1)
+        fin_store(0)
         fin_store(1)

@@ -29,7 +29,7 @@ def tile_conduitdecoder_pa_kernel(
         const = ctx.enter_context(tc.tile_pool(name="const", bufs=1))
         keep = ctx.enter_context(tc.tile_pool(name="keep", bufs=1))
         setup = ctx.enter_context(tc.tile_pool(name="setup", bufs=1))
-        wrp = ctx.enter_context(tc.tile_pool(name="wrp", bufs=3))
+        wrp = ctx.enter_context(tc.tile_pool(name="wrp", bufs=4))
         wgp = ctx.enter_context(tc.tile_pool(name="wgp", bufs=3))
         xgp = ctx.enter_context(tc.tile_pool(name="xgp", bufs=2))
         zbp = ctx.enter_context(tc.tile_pool(name="zbp", bufs=3))
@@ -130,20 +130,22 @@ def tile_conduitdecoder_pa_kernel(
         )
         load_u_high(0)
         load_vt(0, 64)
+        load_wf(0)
         load_u(1)
         load_vt(64, 256)
+        load_wf(1)
         load_u(2)
         load_u_high(1)
-        load_u(3)
-        load_u(4)
-        load_u_high(2)
-        load_u(5)
-        load_u(6)
-        load_u_high(3)
-        load_u(7)
-        load_wf(0)
-        load_wf(1)
         load_wf(2)
+        load_u(3)
+        load_wf(3)
+
+        def late_loads(i):
+            if i < 4:
+                load_u(4 + i)
+                if i % 2 == 0:
+                    load_u_high(2 + i // 2)
+                load_wf(4 + i)
 
         WpC = const.tile([P, H], U32, name="WpC", align_bytes=64)
         WpS = const.tile([P, H], U8, name="WpS", align_bytes=64)
@@ -211,10 +213,8 @@ def tile_conduitdecoder_pa_kernel(
                         nc.tensor.transpose(out=pt[:, u, P * a:P * a + P], in_=wr32[:, 2 * hh + a, w0:w0 + P], identity=identF[:])
                 tiles.append(pt)
             wps[k] = tiles
-            if half == 1 and c + 3 < 8:
-                load_wf(c + 3)
 
-        def w_copies(k, second_on_vector=False):
+        def w_copies(k, second_on_vector):
             wg = wgp.tile([P, H, 4], BF16, name="wg", tag="wg", align_bytes=64)
             wg32 = wg[:].rearrange("p n t -> p (n t)").bitcast(F32).rearrange("p (n u) -> p n u", u=2)
             for hh in range(2):
@@ -228,7 +228,7 @@ def tile_conduitdecoder_pa_kernel(
         def w_quantise(k):
             nc.vector.quantize_mx(out=WC[:, k, :].bitcast(FP8X4), scales=WS[:, k, :], in_=wgs[k][:].rearrange("p n t -> p (n t)"))
 
-        xgs, xcs, zs, gs, ns, nTs, sts, nms, nbs, rss, mps = {}, {}, {}, {}, {}, {}, {}, {}, {}, {}, {}
+        xgs, xcs, zs, gs, ns, nTs, sts, nbs, rss, mps = {}, {}, {}, {}, {}, {}, {}, {}, {}, {}
 
         def x_regroup(s):
             xg = xgp.tile([P, H, 4], BF16, name="xg", align_bytes=64)
@@ -253,48 +253,50 @@ def tile_conduitdecoder_pa_kernel(
             )
             zs[(s, r)] = z
 
-        sgs, sss = {}, {}
+        mvs, sgs, sss = {}, {}, {}
 
         def bias_gelu(s, r):
             zb = zbp.tile([P, H], F32, name="zb")
             nc.vector.tensor_tensor(out=zb[:], in0=zs[(s, r)][:], in1=bpB[:], op=ALU.add)
             g = gpl.tile([P, H], F32, name="g")
-            if r == 3:
+            if r == 0:
                 sgs[s] = small.tile([P, 1], F32, name="sg")
                 nc.scalar.activation(out=g[:], in_=zb[:], func=ACT.Gelu, accum_out=sgs[s][:])
-                nms[s] = small.tile([P, 4], F32, name="nm4")
-                nc.gpsimd.tensor_scalar(out=nms[s][:, 3:4], in0=sgs[s][:], scalar1=-1.0 / H, scalar2=None, op0=ALU.mult)
             else:
                 nc.scalar.activation(out=g[:], in_=zb[:], func=ACT.Gelu)
             gs[(s, r)] = g
+
+        def mean0(s):
+            mvs[s] = small.tile([P, 4, 2], F32, name="mv4")
+            nc.vector.tensor_scalar(out=mvs[s][:, 0, 0:1], in0=sgs[s][:], scalar1=1.0 / H, scalar2=None, op0=ALU.mult)
 
         def square_sum(s):
             junk = junkp.tile([P, H], BF16, name="junk")
             sss[s] = small.tile([P, 1], F32, name="ss")
             nc.scalar.activation(
-                out=junk[:], in_=gs[(s, 3)][:], func=ACT.Square, bias=nms[s][:, 3:4], scale=1.0, accum_out=sss[s][:],
+                out=junk[:], in_=gs[(s, 0)][:], func=ACT.Square, bias=mvs[s][:, 0, 0:1], scale=-1.0, accum_out=sss[s][:],
             )
 
         def stats(s, r):
-            if r == 0:
-                sts[s] = small.tile([P, 3, 6], F32, name="st4")
+            if r == 1:
+                sts[s] = small.tile([P, 4, 6], F32, name="st4")
             nc.vector.bn_stats(out=sts[s][:, r, :], in_=gs[(s, r)][:])
 
         def stats_end(s):
-            mv = small.tile([P, 3, 2], F32, name="mv4")
-            for r in range(3):
+            mv = mvs[s]
+            for r in range(1, 4):
                 nc.vector.bn_aggr(out=mv[:, r, :], in_=sts[s][:, r, :])
-            nm = nms[s]
             ve = small.tile([P, 4], F32, name="ve4")
-            nc.gpsimd.tensor_scalar(out=ve[:, 0:3], in0=mv[:, :, 1], scalar1=EPS, scalar2=None, op0=ALU.add)
-            nc.gpsimd.tensor_scalar(out=ve[:, 3:4], in0=sss[s][:], scalar1=1.0 / H, scalar2=EPS, op0=ALU.mult, op1=ALU.add)
-            nc.gpsimd.tensor_scalar(out=nm[:, 0:3], in0=mv[:, :, 0], scalar1=-1.0, scalar2=None, op0=ALU.mult)
+            nc.vector.tensor_scalar(out=ve[:, 1:4], in0=mv[:, 1:4, 1], scalar1=EPS, scalar2=None, op0=ALU.add)
+            nc.vector.tensor_scalar(out=ve[:, 0:1], in0=sss[s][:], scalar1=1.0 / H, scalar2=EPS, op0=ALU.mult, op1=ALU.add)
             rs = small.tile([P, 4], F32, name="rs4")
             nc.gpsimd.tensor_tensor(out=rs[:], in0=ve[:], in1=neghalf[:], op=ALU.pow)
-            nb = small.tile([P, 4], F32, name="nb4")
-            nc.gpsimd.tensor_tensor(out=nb[:], in0=nm[:], in1=rs[:], op=ALU.mult)
-            nbs[s] = nb
             rss[s] = rs
+
+        def shift(s):
+            nb = small.tile([P, 4], F32, name="nb4")
+            nc.vector.scalar_tensor_tensor(out=nb[:], in0=mvs[s][:, :, 0], scalar=-1.0, in1=rss[s][:], op0=ALU.mult, op1=ALU.mult)
+            nbs[s] = nb
 
         def normalise(s, r, eng):
             n = npl.tile([P, H], F32, name="n")
@@ -341,8 +343,8 @@ def tile_conduitdecoder_pa_kernel(
 
         def m_quantise(bh, kg):
             if kg == 0:
-                MC = keep.tile([P, D, P], U32, name="MC", tag="MC", align_bytes=64, bufs=2)
-                MS = keep.tile([P, D, P], U8, name="MS", tag="MS", align_bytes=64, bufs=2)
+                MC = keep.tile([P, D, P], U32, name="MC", tag="MC", align_bytes=64)
+                MS = keep.tile([P, D, P], U8, name="MS", tag="MS", align_bytes=64)
                 MCs[bh] = (MC, MS)
             MC, MS = MCs[bh]
             nc.vector.quantize_mx(
@@ -376,7 +378,7 @@ def tile_conduitdecoder_pa_kernel(
             mv = small.tile([P, 2], F32, name="mvf")
             nc.vector.bn_aggr(out=mv[:], in_=st[:])
             ve = small.tile([P, 1], F32, name="vef")
-            nc.gpsimd.tensor_scalar(out=ve[:], in0=mv[:, 1:2], scalar1=EPS, scalar2=None, op0=ALU.add)
+            nc.vector.tensor_scalar(out=ve[:], in0=mv[:, 1:2], scalar1=EPS, scalar2=None, op0=ALU.add)
             rs = small.tile([P, 1], F32, name="rsf")
             nc.gpsimd.tensor_tensor(out=rs[:], in0=ve[:], in1=neghalf[:, 0:1], op=ALU.pow)
             o1 = npl.tile([P, H], F32, name="o1", tag="n")
@@ -392,85 +394,86 @@ def tile_conduitdecoder_pa_kernel(
         x_regroup(0)
         spread_bp()
         x_quantise(0)
+        next_w = 0
+        p = None
+        last = NS - 1
         for i in range(NS):
             j = i - 1
-            if j >= 0:
-                normalise(j, 3, "gpsimd")
+            q = next_w
+            next_w += 1
+            if p is not None:
+                w_copies(p, False)
             mx1(i, 0)
             mx1(i, 1)
             bias_gelu(i, 0)
             bias_gelu(i, 1)
             mx1(i, 2)
             mx1(i, 3)
-            if j >= 1:
-                m_regroup(j - 1, 0, D)
-            if j - 1 == 3:
-                m_quantise(0, 0)
-                m_quantise(0, 1)
+            w_transposes(q)
+            if j >= 0:
+                shift(j)
+                normalise(j, 3, "gpsimd")
+            if p is not None:
+                w_quantise(p)
+            mean0(i)
             if j >= 0:
                 for r in range(3):
                     normalise(j, r, "scalar")
                     n_transposes(j, r)
                 n_transposes(j, 3)
+            square_sum(i)
             bias_gelu(i, 2)
             bias_gelu(i, 3)
-            square_sum(i)
+            w_copies(q, False)
+            p = next_w
+            next_w += 1
+            w_transposes(p)
+            late_loads(i)
+            if i == last:
+                mx2(0, 0, 6)
             if i == 0:
                 spread_rest()
-            if i == NS - 1:
-                w_transposes(0)
-                w_copies(0)
-                w_transposes(1)
             if i + 1 < NS:
                 x_regroup(i + 1)
-            stats(i, 0)
             stats(i, 1)
+            stats(i, 2)
             if i + 1 < NS:
                 x_quantise(i + 1)
-            stats(i, 2)
+            stats(i, 3)
             stats_end(i)
+            w_quantise(q)
+            if j >= 1 and i < last:
+                m_regroup(j - 1, 0, D)
             if j - 1 == 3:
-                m_quantise(0, 2)
-                m_quantise(0, 3)
+                for kg in range(4):
+                    m_quantise(0, kg)
             if j >= 0:
                 for t in range(4):
                     affine(j, t, False)
 
-        last = NS - 1
-        w_copies(1)
-        w_transposes(2)
-        m_regroup(last - 1, 0, D)
+        w_copies(p, False)
+        shift(last)
         for r in range(4):
             normalise(last, r, "vector")
             n_transposes(last, r)
-        w_quantise(0)
-        w_quantise(1)
-        mx2(0, 0, 2)
-        w_copies(2)
-        w_transposes(3)
+        m_regroup(last - 2, 0, D)
+        m_regroup(last - 1, 0, D)
+        w_quantise(p)
+        mx2(0, 6, D)
         affine(last, 0, False)
         affine(last, 1, False)
-        affine(last, 2, True)
+        affine(last, 2, False)
         affine(last, 3, True)
-        w_copies(3)
-        w_transposes(4)
         m_regroup(last, 0, 8)
         m_quantise(1, 0)
+        mx2(1, 0, 4)
         m_regroup(last, 8, D)
         for kg in range(1, 4):
             m_quantise(1, kg)
-        mx2(1, 0, 2)
-        for k in range(2, D):
-            w_quantise(k)
-            mx2(0, k, k + 1)
-            mx2(1, k, k + 1)
-            if k + 2 < D:
-                w_copies(k + 2)
-            if k + 3 < D:
-                w_transposes(k + 3)
+            mx2(1, 4 * kg, 4 * kg + 4)
         fin_gelu(0)
-        fin_gelu(1)
         fin_stats(0)
-        fin_stats(1)
+        fin_gelu(1)
         fin_store(0)
+        fin_stats(1)
         fin_store(1)

@@ -108,16 +108,10 @@ def tile_conduitdecoder_pa_kernel(
         nc.gpsimd.dma_start(out=GV[2:4, :], in_=betap.rearrange("(r c) -> r c", r=2))
         identB = const.tile([P, P], BF16, name="identB")
         make_identity(nc, identB[:])
-        for i, vec in ((1, gf), (2, betaf), (3, bfuse)):
-            nc.gpsimd.dma_start(out=VEC[0:1, i, :], in_=vec.rearrange("(o n) -> o n", o=1))
-        nc.gpsimd.dma_start(out=WtIn[:, :, 0:2], in_=wf_rows[:, :, DH:DH + 2])
-        nc.gpsimd.dma_start(out=RA[0:1, :], in_=refine_res.rearrange("(o n) -> o n", o=1))
-        nc.gpsimd.dma_start(out=RA[1:2, :], in_=release_res.rearrange("(o n) -> o n", o=1))
 
         VtB = setup.tile([P, 4, 2, 4, D], BF16, name="VtB")
         vta = VtA[:].rearrange("p (x k q j) -> p q x j k", x=2, k=D, q=4)
-        for q in range(4):
-            nc.vector.tensor_copy(out=VtB[:, q, :, :, :], in_=vta[:, q])
+        nc.vector.tensor_copy(out=VtB[:], in_=vta)
         for q in range(4):
             nc.scalar.activation(
                 out=XR[96:128, 64 * q:64 * q + 64, 0, :],
@@ -130,6 +124,11 @@ def tile_conduitdecoder_pa_kernel(
         )
         load_u_high(0)
         load_vt(0, 64)
+        nc.scalar.dma_start(out=WtIn[:, :, 0:2], in_=wf_rows[:, :, DH:DH + 2])
+        nc.scalar.dma_start(out=RA[0:1, :], in_=refine_res.rearrange("(o n) -> o n", o=1))
+        nc.scalar.dma_start(out=RA[1:2, :], in_=release_res.rearrange("(o n) -> o n", o=1))
+        for i, vec in ((3, bfuse), (1, gf), (2, betaf)):
+            nc.scalar.dma_start(out=VEC[0:1, i, :], in_=vec.rearrange("(o n) -> o n", o=1))
         load_wf(0)
         load_u(1)
         load_vt(64, 256)
@@ -169,7 +168,7 @@ def tile_conduitdecoder_pa_kernel(
         Rsb = const.tile([P, 2, H], F32, name="Rsb")
 
         def spread_bp():
-            pb = psum.tile([P, H], F32, name="pb", tag="nT0")
+            pb = psum.tile([P, H], F32, name="pb", tag="z", bufs=2)
             nc.tensor.matmul(out=pb[:], lhsT=ones[:], rhs=VEC[:, 0, :], start=True, stop=True)
             nc.vector.tensor_copy(
                 out=bpB[:].rearrange("p (u e q) -> p u e q", u=2, e=2),
@@ -177,24 +176,24 @@ def tile_conduitdecoder_pa_kernel(
             )
 
         def spread_rest():
-            pg = psum.tile([P, P], F32, name="pg", tag="nT1")
-            nc.tensor.transpose(out=pg[:], in_=GV[:].bitcast(F32), identity=identF[:])
-            nc.scalar.copy(out=GB[:], in_=pg[:, 0:4].bitcast(BF16))
+            pB = psum.tile([P, H], BF16, name="pB", tag="nT0")
+            for a in range(4):
+                nc.tensor.transpose(out=pB[:, P * a:P * a + P], in_=WtIn[:, a, :], identity=identB[:])
+            nc.scalar.copy(out=RB[:], in_=pB[:])
+            for bh in range(2):
+                pr = psum.tile([P, H], F32, name="pr", tag="wT", bufs=2)
+                nc.tensor.matmul(out=pr[:], lhsT=ones[:], rhs=VEC[:, 3, :], start=True, stop=False)
+                nc.tensor.matmul(out=pr[:], lhsT=RA[:, P * bh:P * bh + P], rhs=RB[:], start=False, stop=True)
+                nc.scalar.copy(out=Rsb[:, bh, :], in_=pr[:])
             pb2 = psum.tile([P, H], F32, name="pb2", tag="nT2")
             nc.tensor.matmul(out=pb2[:], lhsT=ones[:], rhs=VEC[:, 1, :], start=True, stop=True)
             nc.scalar.copy(out=gfB[:], in_=pb2[:])
             pb3 = psum.tile([P, H], F32, name="pb3", tag="nT3")
             nc.tensor.matmul(out=pb3[:], lhsT=ones[:], rhs=VEC[:, 2, :], start=True, stop=True)
             nc.scalar.copy(out=betafB[:], in_=pb3[:])
-            pB = psum.tile([P, H], BF16, name="pB", tag="nT0")
-            for a in range(4):
-                nc.tensor.transpose(out=pB[:, P * a:P * a + P], in_=WtIn[:, a, :], identity=identB[:])
-            nc.scalar.copy(out=RB[:], in_=pB[:])
-            for bh in range(2):
-                pr = psum.tile([P, H], F32, name="pr", tag="nT%d" % (1 + bh))
-                nc.tensor.matmul(out=pr[:], lhsT=ones[:], rhs=VEC[:, 3, :], start=True, stop=False)
-                nc.tensor.matmul(out=pr[:], lhsT=RA[:, P * bh:P * bh + P], rhs=RB[:], start=False, stop=True)
-                nc.scalar.copy(out=Rsb[:, bh, :], in_=pr[:])
+            pg = psum.tile([P, P], F32, name="pg", tag="nT1")
+            nc.tensor.transpose(out=pg[:], in_=GV[:].bitcast(F32), identity=identF[:])
+            nc.scalar.copy(out=GB[:], in_=pg[:, 0:4].bitcast(BF16))
 
         WC = keep.tile([P, D, H], U32, name="WC", align_bytes=64)
         WS = keep.tile([P, D, H], U8, name="WS", align_bytes=64)
@@ -391,8 +390,9 @@ def tile_conduitdecoder_pa_kernel(
             nc.vector.scalar_tensor_tensor(out=o2[:], in0=o1[:], scalar=rs[:], in1=betafB[:], op0=ALU.mult, op1=ALU.add)
             nc.sync.dma_start(out=out[P * bh:P * bh + P, :], in_=o2[:])
 
-        x_regroup(0)
         spread_bp()
+        spread_rest()
+        x_regroup(0)
         x_quantise(0)
         next_w = 0
         p = None
@@ -412,14 +412,16 @@ def tile_conduitdecoder_pa_kernel(
             w_transposes(q)
             if j >= 0:
                 shift(j)
+                normalise(j, 2, "gpsimd")
                 normalise(j, 3, "gpsimd")
             if p is not None:
                 w_quantise(p)
             mean0(i)
             if j >= 0:
-                for r in range(3):
+                for r in range(2):
                     normalise(j, r, "scalar")
                     n_transposes(j, r)
+                n_transposes(j, 2)
                 n_transposes(j, 3)
             square_sum(i)
             bias_gelu(i, 2)
@@ -431,8 +433,6 @@ def tile_conduitdecoder_pa_kernel(
             late_loads(i)
             if i == last:
                 mx2(0, 0, 6)
-            if i == 0:
-                spread_rest()
             if i + 1 < NS:
                 x_regroup(i + 1)
             stats(i, 1)
@@ -442,11 +442,14 @@ def tile_conduitdecoder_pa_kernel(
             stats(i, 3)
             stats_end(i)
             w_quantise(q)
+            if j - 1 == 4:
+                m_quantise(0, 2)
+                m_quantise(0, 3)
             if j >= 1 and i < last:
                 m_regroup(j - 1, 0, D)
             if j - 1 == 3:
-                for kg in range(4):
-                    m_quantise(0, kg)
+                m_quantise(0, 0)
+                m_quantise(0, 1)
             if j >= 0:
                 for t in range(4):
                     affine(j, t, False)
@@ -462,7 +465,7 @@ def tile_conduitdecoder_pa_kernel(
         mx2(0, 6, D)
         affine(last, 0, False)
         affine(last, 1, False)
-        affine(last, 2, False)
+        affine(last, 2, True)
         affine(last, 3, True)
         m_regroup(last, 0, 8)
         m_quantise(1, 0)

from contextlib import ExitStack

import concourse.mybir as mybir
from concourse.masks import make_identity

F32 = mybir.dt.float32
BF16 = mybir.dt.bfloat16
U32 = mybir.dt.uint32
U8 = mybir.dt.uint8
FP8X4 = mybir.dt.float8_e4m3fn_x4
ACT = mybir.ActivationFunctionType
ALU = mybir.AluOpType

P = 128
BN, V, D, H = 256, 491, 16, 512
DH = D * H
FLOPS = 2 * BN * D * H * H + 2 * BN * DH * H
EPS = 1e-5
NS = 8


def tile_conduitdecoder_pa_kernel(
    tc, U, S, Vt, friction, settle, char_coeffs, ext_order, refine_res, release_res,
    Wp, bp, gp, betap, Wf, bfuse, gf, betaf, out,
):
    nc = tc.nc
    with ExitStack() as ctx:
        ctx.enter_context(tc.manual_schedule())
        const = ctx.enter_context(tc.tile_pool(name="const", bufs=1))
        keep = ctx.enter_context(tc.tile_pool(name="keep", bufs=1))
        setup = ctx.enter_context(tc.tile_pool(name="setup", bufs=1))
        wrp = ctx.enter_context(tc.tile_pool(name="wrp", bufs=4))
        wgp = ctx.enter_context(tc.tile_pool(name="wgp", bufs=3))
        xgp = ctx.enter_context(tc.tile_pool(name="xgp", bufs=2))
        zbp = ctx.enter_context(tc.tile_pool(name="zbp", bufs=3))
        gpl = ctx.enter_context(tc.tile_pool(name="gpl", bufs=8))
        npl = ctx.enter_context(tc.tile_pool(name="npl", bufs=4))
        mpp = ctx.enter_context(tc.tile_pool(name="mpp", bufs=2))
        small = ctx.enter_context(tc.tile_pool(name="small", bufs=2))
        junkp = ctx.enter_context(tc.tile_pool(name="junkp", bufs=1))
        psum = ctx.enter_context(tc.psum_pool(name="psum", bufs=1))

        identF = const.tile([P, P], F32, name="identF")
        make_identity(nc, identF[:])
        XR = keep.tile([P, BN, 4, D], BF16, name="XR")
        FR = setup.tile([P, BN * D], BF16, name="FR")
        VtA = setup.tile([P, 2 * D * D], BF16, name="VtA")
        VEC = setup.tile([P, 4, H], BF16, name="VEC")
        GV = setup.tile([P, 256], BF16, name="GV")
        RA = setup.tile([P, BN], BF16, name="RA")
        WtIn = setup.tile([P, 4, P], BF16, name="WtIn")
        ones = const.tile([P, P], BF16, name="ones")
        neghalf = const.tile([P, 4], F32, name="neghalf")
        nc.vector.memset(FR[96:127, :], 0.0)
        nc.vector.memset(VEC[:], 0.0)
        nc.vector.memset(GV[:], 0.0)
        nc.vector.memset(ones[:], 1.0)
        nc.vector.memset(RA[:], 0.0)
        nc.vector.memset(WtIn[:], 0.0)
        nc.vector.memset(neghalf[:], -0.5)

        wf_rows = Wf.rearrange("(a p) c -> p a c", p=P)
        out_flat = out.rearrange("a b -> (a b)")
        WRt = []

        def load_wf(c):
            wr = wrp.tile([P, 4, 1024], BF16, name="wr")
            nc.sync.dma_start(out=wr[:], in_=wf_rows[:, :, 1024 * c:1024 * c + 1024])
            WRt.append(wr)

        def load_u(s):
            nc.sync.dma_start(
                out=XR[0:96, 32 * s:32 * s + 32, :, :].rearrange("p b j k -> p b (j k)"),
                in_=U[32 * s:32 * s + 32, 0:384, :].rearrange("b (p j) k -> p b (j k)", j=4),
            )

        def load_u_high(q):
            b0, b1 = 64 * q, 64 * q + 64
            for (p0, p1, v0, v1) in ((96, 120, 384, 480), (120, 122, 480, 488)):
                nc.sync.dma_start(
                    out=XR[p0:p1, b0:b1, :, :].rearrange("p b j k -> p b (j k)"),
                    in_=U[b0:b1, v0:v1, :].rearrange("b (p j) k -> p b (j k)", j=4),
                )
            nc.sync.dma_start(
                out=XR[122:123, b0:b1, 0:3, :].rearrange("p b j k -> p b (j k)"),
                in_=U[b0:b1, 488:491, :].rearrange("b (p j) k -> p b (j k)", p=1),
            )

        def load_vt(b0, b1):
            nc.sync.dma_start(
                out=XR[123:127, b0:b1, :, :].rearrange("p b j k -> p (b j k)").bitcast(F32),
                in_=out_flat[0:32768].rearrange("(q n) -> q n", q=4)[:, 32 * b0:32 * b1],
            )

        nc.sync.dma_start(out=FR[127:128, :], in_=friction.rearrange("(o b) k -> o (b k)", o=1))
        nc.sync.dma_start(out=VtA[:], in_=Vt.rearrange("(p x) k d -> p (x k d)", x=2))
        WpSb = wgp.tile([P, 4, H], BF16, name="WpSb", tag="wg", align_bytes=64)
        for u in range(2):
            nc.sync.dma_start(
                out=WpSb[:, 2 * u:2 * u + 2, :],
                in_=Wp[256 * u:256 * u + 256, :].rearrange("(p e) i -> p e i", e=2),
            )
        load_u(0)
        for (pp, j, vec) in ((122, 3, S), (127, 1, settle), (127, 2, char_coeffs), (127, 3, ext_order)):
            nc.gpsimd.dma_start(out=XR[pp:pp + 1, :, j, :], in_=vec.rearrange("(o b) k -> o b k", o=1))
        nc.gpsimd.dma_start(out=VEC[0:1, 0, :], in_=bp.rearrange("(o n) -> o n", o=1))
        nc.gpsimd.dma_start(out=GV[0:2, :], in_=gp.rearrange("(r c) -> r c", r=2))
        nc.gpsimd.dma_start(out=GV[2:4, :], in_=betap.rearrange("(r c) -> r c", r=2))
        identB = const.tile([P, P], BF16, name="identB")
        make_identity(nc, identB[:])

        VtB = setup.tile([P, 4, 2, 4, D], BF16, name="VtB")
        vta = VtA[:].rearrange("p (x k q j) -> p q x j k", x=2, k=D, q=4)
        nc.vector.tensor_copy(out=VtB[:], in_=vta)
        for q in range(4):
            nc.scalar.activation(
                out=XR[96:128, 64 * q:64 * q + 64, 0, :],
                in_=FR[96:128, 1024 * q:1024 * q + 1024].rearrange("p (b k) -> p b k", k=D),
                func=ACT.Ln, bias=1.0, scale=1.0,
            )
        nc.sync.dma_start(
            out=out_flat[0:32768].rearrange("(q p w) -> p q w", q=4, p=P),
            in_=VtB[:].rearrange("p q x j k -> p (q x j k)").bitcast(F32).rearrange("p (q w) -> p q w", q=4),
        )
        load_u_high(0)
        load_vt(0, 64)
        nc.scalar.dma_start(out=WtIn[:, :, 0:2], in_=wf_rows[:, :, DH:DH + 2])
        nc.scalar.dma_start(out=RA[0:1, :], in_=refine_res.rearrange("(o n) -> o n", o=1))
        nc.scalar.dma_start(out=RA[1:2, :], in_=release_res.rearrange("(o n) -> o n", o=1))
        for i, vec in ((3, bfuse), (1, gf), (2, betaf)):
            nc.scalar.dma_start(out=VEC[0:1, i, :], in_=vec.rearrange("(o n) -> o n", o=1))
        load_wf(0)
        load_u(1)
        load_vt(64, 256)
        load_wf(1)
        load_u(2)
        load_u_high(1)
        load_wf(2)
        load_u(3)
        load_wf(3)

        def late_loads(i):
            if i < 4:
                load_u(4 + i)
                if i % 2 == 0:
                    load_u_high(2 + i // 2)
                load_wf(4 + i)

        WpC = const.tile([P, H], U32, name="WpC", align_bytes=64)
        WpS = const.tile([P, H], U8, name="WpS", align_bytes=64)
        WpG = wgp.tile([P, H, 4], BF16, name="WpG", tag="wg", align_bytes=64)
        wp32 = WpSb[:].rearrange("p a i -> p (a i)").bitcast(F32).rearrange("p (a q w) -> p a q w", a=4, w=2)
        wpg32 = WpG[:].rearrange("p n t -> p (n t)").bitcast(F32).rearrange("p (n w) -> p n w", w=2)
        for hh in range(2):
            pt = psum.tile([P, 2, 256], F32, name="pt", tag="wT", bufs=2)
            for w in range(2):
                for a in range(2):
                    nc.tensor.transpose(out=pt[:, w, P * a:P * a + P], in_=wp32[:, 2 * hh + a, :, w], identity=identF[:])
            nc.vector.tensor_copy(out=wpg32[:, 256 * hh:256 * hh + 256, :], in_=pt[:].rearrange("p w n -> p n w"))

        nc.vector.quantize_mx(out=WpC[:].bitcast(FP8X4), scales=WpS[:], in_=WpG[:].rearrange("p n t -> p (n t)"))

        bpB = const.tile([P, H], F32, name="bpB")
        gfB = const.tile([P, H], F32, name="gfB")
        betafB = const.tile([P, H], F32, name="betafB")
        GB = const.tile([P, 8], F32, name="GB")
        RB = setup.tile([P, H], BF16, name="RB")
        Rsb = const.tile([P, 2, H], F32, name="Rsb")

        def spread_bp():
            pb = psum.tile([P, H], F32, name="pb", tag="z", bufs=2)
            nc.tensor.matmul(out=pb[:], lhsT=ones[:], rhs=VEC[:, 0, :], start=True, stop=True)
            nc.vector.tensor_copy(
                out=bpB[:].rearrange("p (u e q) -> p u e q", u=2, e=2),
                in_=pb[:].rearrange("p (u q e) -> p u e q", u=2, e=2),
            )

        def spread_rest():
            pB = psum.tile([P, H], BF16, name="pB", tag="nT0")
            for a in range(4):
                nc.tensor.transpose(out=pB[:, P * a:P * a + P], in_=WtIn[:, a, :], identity=identB[:])
            nc.scalar.copy(out=RB[:], in_=pB[:])
            for bh in range(2):
                pr = psum.tile([P, H], F32, name="pr", tag="wT", bufs=2)
                nc.tensor.matmul(out=pr[:], lhsT=ones[:], rhs=VEC[:, 3, :], start=True, stop=False)
                nc.tensor.matmul(out=pr[:], lhsT=RA[:, P * bh:P * bh + P], rhs=RB[:], start=False, stop=True)
                nc.scalar.copy(out=Rsb[:, bh, :], in_=pr[:])
            pb2 = psum.tile([P, H], F32, name="pb2", tag="nT2")
            nc.tensor.matmul(out=pb2[:], lhsT=ones[:], rhs=VEC[:, 1, :], start=True, stop=True)
            nc.scalar.copy(out=gfB[:], in_=pb2[:])
            pb3 = psum.tile([P, H], F32, name="pb3", tag="nT3")
            nc.tensor.matmul(out=pb3[:], lhsT=ones[:], rhs=VEC[:, 2, :], start=True, stop=True)
            nc.scalar.copy(out=betafB[:], in_=pb3[:])
            pg = psum.tile([P, P], F32, name="pg", tag="nT1")
            nc.tensor.transpose(out=pg[:], in_=GV[:].bitcast(F32), identity=identF[:])
            nc.scalar.copy(out=GB[:], in_=pg[:, 0:4].bitcast(BF16))

        WC = keep.tile([P, D, H], U32, name="WC", align_bytes=64)
        WS = keep.tile([P, D, H], U8, name="WS", align_bytes=64)
        wps = {}
        wgs = {}

        def w_transposes(k):
            c, half = divmod(k, 2)
            wr32 = WRt[c][:].rearrange("p a c -> p (a c)").bitcast(F32).rearrange("p (a w) -> p a w", a=4)
            tiles = []
            for hh in range(2):
                pt = psum.tile([P, 2, 256], F32, name="pt", tag="wT", bufs=2)
                for u in range(2):
                    for a in range(2):
                        w0 = 256 * half + P * u
                        nc.tensor.transpose(out=pt[:, u, P * a:P * a + P], in_=wr32[:, 2 * hh + a, w0:w0 + P], identity=identF[:])
                tiles.append(pt)
            wps[k] = tiles

        def w_copies(k, second_on_vector):
            wg = wgp.tile([P, H, 4], BF16, name="wg", tag="wg", align_bytes=64)
            wg32 = wg[:].rearrange("p n t -> p (n t)").bitcast(F32).rearrange("p (n u) -> p n u", u=2)
            for hh in range(2):
                src = wps[k][hh][:].rearrange("p u n -> p n u")
                if hh == 1 and second_on_vector:
                    nc.vector.tensor_copy(out=wg32[:, 256 * hh:256 * hh + 256, :], in_=src)
                else:
                    nc.scalar.copy(out=wg32[:, 256 * hh:256 * hh + 256, :], in_=src)
            wgs[k] = wg

        def w_quantise(k):
            nc.vector.quantize_mx(out=WC[:, k, :].bitcast(FP8X4), scales=WS[:, k, :], in_=wgs[k][:].rearrange("p n t -> p (n t)"))

        xgs, xcs, zs, gs, ns, nTs, sts, nbs, rss, mps = {}, {}, {}, {}, {}, {}, {}, {}, {}, {}

        def x_regroup(s):
            xg = xgp.tile([P, H, 4], BF16, name="xg", align_bytes=64)
            nc.vector.tensor_copy(
                out=xg[:].rearrange("p (b c i) j -> p b c j i", c=4, i=4),
                in_=XR[:, 32 * s:32 * s + 32, :, :].rearrange("p b j (c i) -> p b c j i", i=4),
            )
            xgs[s] = xg

        def x_quantise(s):
            xc = xgp.tile([P, H], U32, name="xc", align_bytes=64)
            xs = xgp.tile([P, H], U8, name="xs", align_bytes=64)
            nc.vector.quantize_mx(out=xc[:].bitcast(FP8X4), scales=xs[:], in_=xgs[s][:].rearrange("p c j -> p (c j)"))
            xcs[s] = (xc, xs)

        def mx1(s, r):
            xc, xs = xcs[s]
            z = psum.tile([P, H], F32, name="z", tag="z", bufs=2)
            nc.tensor.matmul_mx(
                out=z[:], lhsT=xc[:, P * r:P * r + P].bitcast(FP8X4), lhsT_scale=xs[:, P * r:P * r + P],
                rhs=WpC[:].bitcast(FP8X4), rhs_scale=WpS[:], start=True, stop=True,
            )
            zs[(s, r)] = z

        mvs, sgs, sss = {}, {}, {}

        def bias_gelu(s, r):
            zb = zbp.tile([P, H], F32, name="zb")
            nc.vector.tensor_tensor(out=zb[:], in0=zs[(s, r)][:], in1=bpB[:], op=ALU.add)
            g = gpl.tile([P, H], F32, name="g")
            if r == 0:
                sgs[s] = small.tile([P, 1], F32, name="sg")
                nc.scalar.activation(out=g[:], in_=zb[:], func=ACT.Gelu, accum_out=sgs[s][:])
            else:
                nc.scalar.activation(out=g[:], in_=zb[:], func=ACT.Gelu)
            gs[(s, r)] = g

        def mean0(s):
            mvs[s] = small.tile([P, 4, 2], F32, name="mv4")
            nc.vector.tensor_scalar(out=mvs[s][:, 0, 0:1], in0=sgs[s][:], scalar1=1.0 / H, scalar2=None, op0=ALU.mult)

        def square_sum(s):
            junk = junkp.tile([P, H], BF16, name="junk")
            sss[s] = small.tile([P, 1], F32, name="ss")
            nc.scalar.activation(
                out=junk[:], in_=gs[(s, 0)][:], func=ACT.Square, bias=mvs[s][:, 0, 0:1], scale=-1.0, accum_out=sss[s][:],
            )

        def stats(s, r):
            if r == 1:
                sts[s] = small.tile([P, 4, 6], F32, name="st4")
            nc.vector.bn_stats(out=sts[s][:, r, :], in_=gs[(s, r)][:])

        def stats_end(s):
            mv = mvs[s]
            for r in range(1, 4):
                nc.vector.bn_aggr(out=mv[:, r, :], in_=sts[s][:, r, :])
            ve = small.tile([P, 4], F32, name="ve4")
            nc.vector.tensor_scalar(out=ve[:, 1:4], in0=mv[:, 1:4, 1], scalar1=EPS, scalar2=None, op0=ALU.add)
            nc.vector.tensor_scalar(out=ve[:, 0:1], in0=sss[s][:], scalar1=1.0 / H, scalar2=EPS, op0=ALU.mult, op1=ALU.add)
            rs = small.tile([P, 4], F32, name="rs4")
            nc.gpsimd.tensor_tensor(out=rs[:], in0=ve[:], in1=neghalf[:], op=ALU.pow)
            rss[s] = rs

        def shift(s):
            nb = small.tile([P, 4], F32, name="nb4")
            nc.vector.scalar_tensor_tensor(out=nb[:], in0=mvs[s][:, :, 0], scalar=-1.0, in1=rss[s][:], op0=ALU.mult, op1=ALU.mult)
            nbs[s] = nb

        def normalise(s, r, eng):
            n = npl.tile([P, H], F32, name="n")
            if eng == "scalar":
                nc.scalar.activation(
                    out=n[:], in_=gs[(s, r)][:], func=ACT.Identity, scale=rss[s][:, r:r + 1], bias=nbs[s][:, r:r + 1],
                )
            else:
                engine = nc.gpsimd if eng == "gpsimd" else nc.vector
                engine.tensor_scalar(
                    out=n[:], in0=gs[(s, r)][:], scalar1=rss[s][:, r:r + 1], scalar2=nbs[s][:, r:r + 1], op0=ALU.mult, op1=ALU.add,
                )
            ns[(s, r)] = n

        def n_transposes(s, r):
            if r == 0:
                nTs[s] = [psum.tile([P, H], F32, name="nT%d" % t, tag="nT%d" % t) for t in range(4)]
            for t in range(4):
                nc.tensor.transpose(out=nTs[s][t][:, P * r:P * r + P], in_=ns[(s, r)][:, P * t:P * t + P], identity=identF[:])

        def affine(s, t, on_vector):
            if t == 0:
                mps[s] = mpp.tile([P, 4, D, 32], BF16, name="mp")
            src = nTs[s][t][:].rearrange("p (rb k) -> p k rb", k=D)
            if on_vector:
                nc.vector.tensor_scalar(
                    out=mps[s][:, t, :, :], in0=src, scalar1=GB[:, t:t + 1], scalar2=GB[:, 4 + t:5 + t], op0=ALU.mult, op1=ALU.add,
                )
            else:
                nc.scalar.activation(
                    out=mps[s][:, t, :, :], in_=src, func=ACT.Identity, scale=GB[:, t:t + 1], bias=GB[:, 4 + t:5 + t],
                )

        MGs, MCs = {}, {}

        def m_regroup(s, k0, k1):
            bh, sl = divmod(s, 4)
            if sl == 0 and k0 == 0:
                MGs[bh] = keep.tile([P, D, P, 4], BF16, name="MG", tag="MG", align_bytes=64)
            nc.vector.tensor_copy(
                out=MGs[bh][:, k0:k1, 32 * sl:32 * sl + 32, :].rearrange("p k (c i) t -> p k c t i", i=4),
                in_=mps[s][:, :, k0:k1, :].rearrange("p t k (c i) -> p k c t i", i=4),
            )

        def m_quantise(bh, kg):
            if kg == 0:
                MC = keep.tile([P, D, P], U32, name="MC", tag="MC", align_bytes=64)
                MS = keep.tile([P, D, P], U8, name="MS", tag="MS", align_bytes=64)
                MCs[bh] = (MC, MS)
            MC, MS = MCs[bh]
            nc.vector.quantize_mx(
                out=MC[:, 4 * kg:4 * kg + 4, :].rearrange("p k b -> p (k b)").bitcast(FP8X4),
                scales=MS[:, 4 * kg:4 * kg + 4, :].rearrange("p k b -> p (k b)"),
                in_=MGs[bh][:, 4 * kg:4 * kg + 4, :, :].rearrange("p k b t -> p (k b t)"),
            )

        accs, fin = {}, {}

        def mx2(bh, k0, k1):
            if k0 == 0:
                accs[bh] = psum.tile([P, H], F32, name="acc", tag="z", bufs=2)
            MC, MS = MCs[bh]
            for k in range(k0, k1):
                nc.tensor.matmul_mx(
                    out=accs[bh][:], lhsT=MC[:, k, :].bitcast(FP8X4), lhsT_scale=MS[:, k, :],
                    rhs=WC[:, k, :].bitcast(FP8X4), rhs_scale=WS[:, k, :], start=(k == 0), stop=(k == D - 1),
                )

        def fin_gelu(bh):
            z2 = zbp.tile([P, H], F32, name="z2", tag="zb")
            nc.vector.tensor_tensor(out=z2[:], in0=accs[bh][:], in1=Rsb[:, bh, :], op=ALU.add)
            g2 = gpl.tile([P, H], F32, name="g2", tag="g")
            nc.scalar.activation(out=g2[:], in_=z2[:], func=ACT.Gelu)
            fin[bh] = g2

        def fin_stats(bh):
            st = small.tile([P, 6], F32, name="stf")
            nc.vector.bn_stats(out=st[:], in_=fin[bh][:])
            mv = small.tile([P, 2], F32, name="mvf")
            nc.vector.bn_aggr(out=mv[:], in_=st[:])
            ve = small.tile([P, 1], F32, name="vef")
            nc.vector.tensor_scalar(out=ve[:], in0=mv[:, 1:2], scalar1=EPS, scalar2=None, op0=ALU.add)
            rs = small.tile([P, 1], F32, name="rsf")
            nc.gpsimd.tensor_tensor(out=rs[:], in0=ve[:], in1=neghalf[:, 0:1], op=ALU.pow)
            o1 = npl.tile([P, H], F32, name="o1", tag="n")
            nc.vector.scalar_tensor_tensor(out=o1[:], in0=fin[bh][:], scalar=mv[:, 0:1], in1=gfB[:], op0=ALU.subtract, op1=ALU.mult)
            fin[bh] = (o1, rs)

        def fin_store(bh):
            o1, rs = fin[bh]
            o2 = zbp.tile([P, H], F32, name="o2", tag="zb")
            nc.vector.scalar_tensor_tensor(out=o2[:], in0=o1[:], scalar=rs[:], in1=betafB[:], op0=ALU.mult, op1=ALU.add)
            nc.sync.dma_start(out=out[P * bh:P * bh + P, :], in_=o2[:])

        spread_bp()
        spread_rest()
        x_regroup(0)
        x_quantise(0)
        next_w = 0
        p = None
        last = NS - 1
        for i in range(NS):
            j = i - 1
            q = next_w
            next_w += 1
            if p is not None:
                w_copies(p, False)
            mx1(i, 0)
            mx1(i, 1)
            bias_gelu(i, 0)
            bias_gelu(i, 1)
            mx1(i, 2)
            mx1(i, 3)
            w_transposes(q)
            if j >= 0:
                shift(j)
                normalise(j, 2, "gpsimd")
                normalise(j, 3, "gpsimd")
            if p is not None:
                w_quantise(p)
            mean0(i)
            if j >= 0:
                for r in range(2):
                    normalise(j, r, "scalar")
                    n_transposes(j, r)
                n_transposes(j, 2)
                n_transposes(j, 3)
            square_sum(i)
            bias_gelu(i, 2)
            bias_gelu(i, 3)
            w_copies(q, False)
            p = next_w
            next_w += 1
            w_transposes(p)
            late_loads(i)
            if i == last:
                mx2(0, 0, 6)
            if i + 1 < NS:
                x_regroup(i + 1)
            stats(i, 1)
            stats(i, 2)
            if i + 1 < NS:
                x_quantise(i + 1)
            stats(i, 3)
            stats_end(i)
            w_quantise(q)
            if j - 1 == 4:
                m_quantise(0, 2)
                m_quantise(0, 3)
            if j >= 1 and i < last:
                m_regroup(j - 1, 0, D)
            if j - 1 == 3:
                m_quantise(0, 0)
                m_quantise(0, 1)
            if j >= 0:
                for t in range(4):
                    affine(j, t, False)

        w_copies(p, False)
        shift(last)
        for r in range(4):
            normalise(last, r, "vector")
            n_transposes(last, r)
        m_regroup(last - 2, 0, D)
        m_regroup(last - 1, 0, D)
        w_quantise(p)
        mx2(0, 6, D)
        affine(last, 0, False)
        affine(last, 1, False)
        affine(last, 2, True)
        affine(last, 3, True)
        m_regroup(last, 0, 8)
        m_quantise(1, 0)
        mx2(1, 0, 4)
        m_regroup(last, 8, D)
        for kg in range(1, 4):
            m_quantise(1, kg)
            mx2(1, 4 * kg, 4 * kg + 4)
        fin_gelu(0)
        fin_stats(0)
        fin_gelu(1)
        fin_store(0)
        fin_stats(1)
        fin_store(1)
